import numpy as np
import ml_dtypes


def mxq(x, axis, fmt="e4m3"):
    dtype, down = {"e4m3": (ml_dtypes.float8_e4m3fn, 7), "e5m2": (ml_dtypes.float8_e5m2, 14)}[fmt]
    v = np.moveaxis(np.asarray(x, np.float32).astype(ml_dtypes.bfloat16).astype(np.float64), axis, -1)
    blocks = v.reshape(v.shape[:-1] + (-1, 32))
    amax = np.abs(blocks).max(-1, keepdims=True)
    byte = np.maximum(np.where(amax > 0, np.frexp(amax)[1] - 1 + 127, 0) - down, 1)
    scale = np.exp2(byte - 127.0)
    codes = (blocks / scale).astype(np.float32).astype(dtype).astype(np.float64)
    return np.moveaxis((codes * scale).reshape(v.shape), -1, axis)


WIDE = False


def mx_kscale(k):
    if not WIDE:
        return np.ones(k)
    levels = np.array([10, -10, 5, -5, 0])
    if k % 512:
        return np.exp2(np.random.permutation(np.resize(levels, k // 32))).repeat(32)
    a = np.empty((k // 512, 16))
    for p in range(k // 512):
        a[p, :8] = np.random.permutation(np.resize(levels, 8))
        for g in range(8):
            far = levels[np.abs(levels - a[p, g]) >= 10]
            a[p, g + 8] = far[np.random.randint(len(far))]
    return np.exp2(a.ravel()).repeat(32)


BF16 = ml_dtypes.bfloat16


def bf(x):
    return np.asarray(x, np.float32).astype(BF16)


def f64(x):
    return np.asarray(x).astype(np.float64)


T, H, I, R = 2048, 1536, 5376, 1024


def silu(v):
    return v / (1.0 + np.exp(-v))


def setup_inputs():
    s, t = mx_kscale(H), mx_kscale(R)
    return {
        "x": bf(np.random.standard_normal((T, H)) * s),
        "Wmean1": bf(np.random.standard_normal((I, H)) / np.sqrt(H) / s),
        "Wmean3": bf(np.random.standard_normal((I, H)) / np.sqrt(H) / s),
        "du1": bf(np.random.standard_normal((I, R)) * 0.5 / np.sqrt(R) / t),
        "dv1": bf(np.random.standard_normal((R, H)) / np.sqrt(H) / s * t[:, None]),
        "du3": bf(np.random.standard_normal((I, R)) * 0.5 / np.sqrt(R) / t),
        "dv3": bf(np.random.standard_normal((R, H)) / np.sqrt(H) / s * t[:, None]),
    }


def reference(x, Wmean1, Wmean3, du1, dv1, du3, dv3):
    xq = mxq(f64(x), 1, "e4m3")
    p3 = xq @ mxq(f64(dv3), 1, "e4m3").T
    up = (xq @ mxq(f64(Wmean3), 1, "e4m3").T) + (mxq(p3, 1, "e4m3") @ mxq(f64(du3), 1, "e4m3").T)
    p1 = xq @ mxq(f64(dv1), 1, "e4m3").T
    gate = (xq @ mxq(f64(Wmean1), 1, "e4m3").T) + (mxq(p1, 1, "e4m3") @ mxq(f64(du1), 1, "e4m3").T)
    return silu(gate) * up

@@ -1,0 +1,252 @@
+from contextlib import ExitStack
+
+import concourse.masks as masks
+import concourse.mybir as mybir
+
+T, H, I, R = 2048, 1536, 5376, 1024
+FLOPS = 2 * T * (2 * H * I + 2 * H * R + 2 * R * I)
+
+F32 = mybir.dt.float32
+BF16 = mybir.dt.bfloat16
+U32 = mybir.dt.uint32
+U8 = mybir.dt.uint8
+FP8X4 = mybir.dt.float8_e4m3fn_x4
+SILU = mybir.ActivationFunctionType.Silu
+MULT = mybir.AluOpType.mult
+
+P = 128
+K_PASS = 512
+CHUNK = 512
+HALF = 256
+H_PASSES = H // K_PASS
+R_PASSES = R // K_PASS
+TOKEN_CHUNKS = T // CHUNK
+TOKEN_TILES = T // P
+I_CHUNKS = (I + CHUNK - 1) // CHUNK
+
+RAW_BUFS = 8
+HEAD_BLOCKS = 15
+STAGE1_BLOCKS = {0: 3, 1: 3, 2: 3, 3: 3, 4: 3, 5: 3, 6: 3, 7: 3, 8: 3, 9: 3, 10: 3, 12: 4, 14: 4, 16: 4, 18: 4, 20: 4}
+RUN_AFTER = (1, 4, 7, 10, 13)
+RUN_BLOCKS = 4
+
+
+def tile_merge_mixtralsparsemoeblock_pa_l_kernel(tc, x, Wmean1, Wmean3, du1, dv1, du3, dv3, out):
+    nc = tc.nc
+    with ExitStack() as ctx:
+        keep = ctx.enter_context(tc.tile_pool(name="keep", bufs=1))
+        rawp = ctx.enter_context(tc.tile_pool(name="rawp", bufs=RAW_BUFS))
+        grpp = ctx.enter_context(tc.tile_pool(name="grpp", bufs=8))
+        wcp = ctx.enter_context(tc.tile_pool(name="wcp", bufs=22))
+        pstp = ctx.enter_context(tc.tile_pool(name="pstp", bufs=2))
+        epi = ctx.enter_context(tc.tile_pool(name="epi", bufs=4))
+        tpp = ctx.enter_context(tc.psum_pool(name="tpp", bufs=4))
+        accp = ctx.enter_context(tc.psum_pool(name="accp", bufs=4))
+
+        ident = keep.tile([P, P], F32, name="ident")
+        masks.make_identity(nc, ident[:])
+        warm_in = keep.tile([P, 8], F32, name="warm_in")
+        warm_out = keep.tile([P, 8], F32, name="warm_out")
+        nc.vector.memset(warm_in[:], 0.0)
+        nc.scalar.activation(out=warm_out[:], in_=warm_in[:], func=SILU)
+
+        ctx.enter_context(tc.manual_schedule())
+
+        x_view = x.rearrange("(a j p) k -> a p j k", j=2, p=P)
+        w_view = (
+            Wmean1.rearrange("(a j p) k -> a p j k", j=2, p=P),
+            Wmean3.rearrange("(a j p) k -> a p j k", j=2, p=P),
+        )
+        du_view = (
+            du1.rearrange("(a j p) k -> a p j k", j=2, p=P),
+            du3.rearrange("(a j p) k -> a p j k", j=2, p=P),
+        )
+        dv_view = (
+            dv1.rearrange("(g m b j) k -> g b m j k", m=P, b=2, j=2),
+            dv3.rearrange("(g m b j) k -> g b m j k", m=P, b=2, j=2),
+        )
+
+        jobs = []
+        for b in range(2):
+            jobs.append((x_view[b], H_PASSES, ("x", 0), b))
+        for i in range(2):
+            for gr in range(R_PASSES):
+                for b in range(2):
+                    jobs.append((dv_view[i][gr, b], H_PASSES, ("dv", i, gr), b))
+        for c in range(1, TOKEN_CHUNKS):
+            for b in range(2):
+                jobs.append((x_view[2 * c + b], H_PASSES, ("x", c), b))
+        for n in range(I_CHUNKS):
+            halves = min(CHUNK, I - n * CHUNK) // HALF
+            for i in range(2):
+                for b in range(halves):
+                    jobs.append((w_view[i][2 * n + b], H_PASSES, ("w", n, i), b))
+            for i in range(2):
+                for b in range(halves):
+                    jobs.append((du_view[i][2 * n + b], R_PASSES, ("du", n, i), b))
+
+        blocks = []
+        loads_after = {}
+        for jb in range(len(jobs)):
+            for g in range(jobs[jb][1]):
+                blocks.append((jb, g))
+            if jb + RAW_BUFS < len(jobs):
+                loads_after[len(blocks) - 1] = jb + RAW_BUFS
+
+        first_block_of_chunk = {}
+        for bi in range(len(blocks)):
+            key = jobs[blocks[bi][0]][2]
+            if key[0] == "w" and key[1] not in first_block_of_chunk:
+                first_block_of_chunk[key[1]] = bi
+        first_block_of_chunk[I_CHUNKS] = len(blocks)
+
+        raw_of = {}
+        grp_of = {}
+        units = {}
+
+        def unit_tiles(key, g):
+            if (key, g) not in units:
+                if key[0] == "x" or key[0] == "p":
+                    label = "%s%d" % (key[0], 100 * key[1] + 10 * key[-1] + g)
+                    codes = keep.tile([P, CHUNK], U32, name="c_" + label, align_bytes=64)
+                    scales = keep.tile([P, CHUNK], U8, name="s_" + label, align_bytes=64)
+                else:
+                    codes = wcp.tile([P, CHUNK], U32, name="wcodes", tag="wcodes", align_bytes=64)
+                    scales = wcp.tile([P, CHUNK], U8, name="wscales", tag="wscales", align_bytes=64)
+                units[(key, g)] = (codes, scales)
+            return units[(key, g)]
+
+        def load(jb):
+            raw = rawp.tile([P, 2, jobs[jb][1] * K_PASS], BF16, name="raw", tag="raw")
+            nc.sync.dma_start(out=raw[:], in_=jobs[jb][0])
+            raw_of[jb] = raw
+
+        def transpose_block(bi):
+            jb, g = blocks[bi]
+            words = raw_of[jb][:].bitcast(F32)
+            tp = tpp.tile([P, 2, 2, P], F32, name="tp", tag="tp")
+            for j in range(2):
+                for u in range(2):
+                    nc.tensor.transpose(tp[:, j, u, :], words[:, j, 256 * g + u : 256 * (g + 1) : 2], ident[:])
+            grp = grpp.tile([P, HALF, 4], BF16, name="grp", tag="grp", align_bytes=64)
+            dst = grp[:].bitcast(F32).rearrange("p (j r) u -> p j r u", j=2)
+            src = tp[:].rearrange("p j u r -> p j r u")
+            on_scalar = (bi % 3 != 2) if bi < first_block_of_chunk[0] else (bi % 2 == 0)
+            if on_scalar:
+                nc.scalar.copy(out=dst, in_=src)
+            else:
+                nc.vector.tensor_copy(out=dst, in_=src)
+            grp_of[bi] = grp
+            if bi in loads_after:
+                load(loads_after[bi])
+
+        def quantize_block(bi):
+            jb, g = blocks[bi]
+            codes, scales = unit_tiles(jobs[jb][2], g)
+            cols = slice(HALF * jobs[jb][3], HALF * (jobs[jb][3] + 1))
+            nc.vector.quantize_mx(
+                out=codes[:, cols].bitcast(FP8X4),
+                scales=scales[:, cols],
+                in_=grp_of[bi][:].rearrange("p r t -> p (r t)"),
+            )
+
+        def p_groups(i, gr, c, h, pst):
+            for t in (2 * h, 2 * h + 1):
+                cols = slice(P * t, P * (t + 1))
+                acc = accp.tile([P, CHUNK], F32, name="acc", tag="acc")
+                for g in range(H_PASSES):
+                    dc, ds = units[(("dv", i, gr), g)]
+                    xc, xs = units[(("x", c), g)]
+                    nc.tensor.matmul_mx(
+                        out=acc[:],
+                        lhsT=dc[:, cols].bitcast(FP8X4),
+                        lhsT_scale=ds[:, cols],
+                        rhs=xc[:].bitcast(FP8X4),
+                        rhs_scale=xs[:],
+                        start=(g == 0),
+                        stop=(g == H_PASSES - 1),
+                    )
+                nc.scalar.copy(out=pst[:, t, :], in_=acc[:])
+
+        def output_tile(n, m):
+            width = min(CHUNK, I - n * CHUNK)
+            c = m // 4
+            tok = slice(P * (m % 4), P * (m % 4 + 1))
+            banks = []
+            for i in range(2):
+                pairs = []
+                for g in range(H_PASSES):
+                    pairs.append((units[(("x", c), g)], units[(("w", n, i), g)]))
+                for gr in range(R_PASSES):
+                    pairs.append((units[(("p", i, gr), c)], units[(("du", n, i), gr)]))
+                acc = accp.tile([P, CHUNK], F32, name="acc", tag="acc")
+                for q in range(len(pairs)):
+                    (ac, asc), (wc, wsc) = pairs[q]
+                    nc.tensor.matmul_mx(
+                        out=acc[:, :width],
+                        lhsT=ac[:, tok].bitcast(FP8X4),
+                        lhsT_scale=asc[:, tok],
+                        rhs=wc[:, :width].bitcast(FP8X4),
+                        rhs_scale=wsc[:, :width],
+                        start=(q == 0),
+                        stop=(q == len(pairs) - 1),
+                    )
+                banks.append(acc)
+            sg = epi.tile([P, CHUNK], F32, name="sg", tag="sg")
+            nc.scalar.activation(out=sg[:, :width], in_=banks[0][:, :width], func=SILU)
+            z = epi.tile([P, CHUNK], F32, name="z", tag="z")
+            nc.vector.tensor_tensor(out=z[:, :width], in0=banks[1][:, :width], in1=sg[:, :width], op=MULT)
+            nc.sync.dma_start(out=out[P * m : P * (m + 1), CHUNK * n : CHUNK * n + width], in_=z[:, :width])
+
+        for jb in range(RAW_BUFS):
+            load(jb)
+        t_next = 0
+        q_next = 0
+        for rep in range(HEAD_BLOCKS):
+            transpose_block(t_next)
+            t_next += 1
+            if t_next - q_next > 2:
+                quantize_block(q_next)
+                q_next += 1
+
+        waiting_p = []
+        pst = None
+        for k in range(2 * 4 * TOKEN_CHUNKS):
+            c = k // 8
+            i = (k % 8) // 4
+            gr = ((k % 8) // 2) % 2
+            h = k % 2
+            while q_next < t_next:
+                quantize_block(q_next)
+                q_next += 1
+            if h == 0:
+                pst = pstp.tile([P, 4, CHUNK], BF16, name="pst", tag="pst")
+            p_groups(i, gr, c, h, pst)
+            for item in waiting_p:
+                pc, psc = unit_tiles(item[1], item[2])
+                nc.vector.quantize_mx(
+                    out=pc[:].bitcast(FP8X4), scales=psc[:], in_=item[0][:].rearrange("p c t -> p (c t)")
+                )
+            waiting_p = []
+            if h == 1:
+                pg = pstp.tile([P, CHUNK, 4], BF16, name="pg", tag="pg", align_bytes=64)
+                nc.vector.tensor_copy(out=pg[:], in_=pst[:].rearrange("p t c -> p c t"))
+                waiting_p.append((pg, ("p", i, gr), c))
+            for rep in range(STAGE1_BLOCKS.get(k, 0)):
+                transpose_block(t_next)
+                t_next += 1
+        for item in waiting_p:
+            pc, psc = unit_tiles(item[1], item[2])
+            nc.vector.quantize_mx(out=pc[:].bitcast(FP8X4), scales=psc[:], in_=item[0][:].rearrange("p c t -> p (c t)"))
+
+        for n in range(I_CHUNKS):
+            for m in range(TOKEN_TILES):
+                output_tile(n, m)
+                while q_next < t_next:
+                    quantize_block(q_next)
+                    q_next += 1
+                if m in RUN_AFTER:
+                    for rep in range(RUN_BLOCKS):
+                        if n + 1 < I_CHUNKS and t_next < first_block_of_chunk[n + 2]:
+                            transpose_block(t_next)
+                            t_next += 1

@@ -29,6 +29,7 @@ HEAD_BLOCKS = 15
 STAGE1_BLOCKS = {0: 3, 1: 3, 2: 3, 3: 3, 4: 3, 5: 3, 6: 3, 7: 3, 8: 3, 9: 3, 10: 3, 12: 4, 14: 4, 16: 4, 18: 4, 20: 4}
 RUN_AFTER = (1, 4, 7, 10, 13)
 RUN_BLOCKS = 4
+SORT_FROM = 48
 
 
 def tile_merge_mixtralsparsemoeblock_pa_l_kernel(tc, x, Wmean1, Wmean3, du1, dv1, du3, dv3, out):
@@ -39,6 +40,7 @@ def tile_merge_mixtralsparsemoeblock_pa_l_kernel(tc, x, Wmean1, Wmean3, du1, dv1
         grpp = ctx.enter_context(tc.tile_pool(name="grpp", bufs=8))
         wcp = ctx.enter_context(tc.tile_pool(name="wcp", bufs=22))
         pstp = ctx.enter_context(tc.tile_pool(name="pstp", bufs=2))
+        srtp = ctx.enter_context(tc.tile_pool(name="srtp", bufs=4))
         epi = ctx.enter_context(tc.tile_pool(name="epi", bufs=4))
         tpp = ctx.enter_context(tc.psum_pool(name="tpp", bufs=4))
         accp = ctx.enter_context(tc.psum_pool(name="accp", bufs=4))
@@ -102,6 +104,7 @@ def tile_merge_mixtralsparsemoeblock_pa_l_kernel(tc, x, Wmean1, Wmean3, du1, dv1
 
         raw_of = {}
         grp_of = {}
+        srt_of = {}
         units = {}
 
         def unit_tiles(key, g):
@@ -121,17 +124,31 @@ def tile_merge_mixtralsparsemoeblock_pa_l_kernel(tc, x, Wmean1, Wmean3, du1, dv1
             nc.sync.dma_start(out=raw[:], in_=jobs[jb][0])
             raw_of[jb] = raw
 
+        def sort_block(bi):
+            if bi < SORT_FROM or bi >= len(blocks):
+                return
+            jb, g = blocks[bi]
+            words = raw_of[jb][:].bitcast(F32)
+            srt = srtp.tile([P, 2, 2, P], F32, name="srt", tag="srt")
+            nc.vector.tensor_copy(
+                out=srt[:], in_=words[:, :, 256 * g : 256 * (g + 1)].rearrange("p j (q u) -> p j u q", u=2)
+            )
+            srt_of[bi] = srt
+
         def transpose_block(bi):
             jb, g = blocks[bi]
             words = raw_of[jb][:].bitcast(F32)
             tp = tpp.tile([P, 2, 2, P], F32, name="tp", tag="tp")
             for j in range(2):
                 for u in range(2):
-                    nc.tensor.transpose(tp[:, j, u, :], words[:, j, 256 * g + u : 256 * (g + 1) : 2], ident[:])
+                    if bi in srt_of:
+                        nc.tensor.transpose(tp[:, j, u, :], srt_of[bi][:, j, u, :], ident[:])
+                    else:
+                        nc.tensor.transpose(tp[:, j, u, :], words[:, j, 256 * g + u : 256 * (g + 1) : 2], ident[:])
             grp = grpp.tile([P, HALF, 4], BF16, name="grp", tag="grp", align_bytes=64)
             dst = grp[:].bitcast(F32).rearrange("p (j r) u -> p j r u", j=2)
             src = tp[:].rearrange("p j u r -> p j r u")
-            on_scalar = (bi % 3 != 2) if bi < first_block_of_chunk[0] else (bi % 2 == 0)
+            on_scalar = (bi % 3 != 2) if bi < first_block_of_chunk[0] else True
             if on_scalar:
                 nc.scalar.copy(out=dst, in_=src)
             else:
@@ -228,6 +245,8 @@ def tile_merge_mixtralsparsemoeblock_pa_l_kernel(tc, x, Wmean1, Wmean3, du1, dv1
                     out=pc[:].bitcast(FP8X4), scales=psc[:], in_=item[0][:].rearrange("p c t -> p (c t)")
                 )
             waiting_p = []
+            for rep in range(STAGE1_BLOCKS.get(k + 1, 0)):
+                sort_block(t_next + STAGE1_BLOCKS.get(k, 0) + rep)
             if h == 1:
                 pg = pstp.tile([P, CHUNK, 4], BF16, name="pg", tag="pg", align_bytes=64)
                 nc.vector.tensor_copy(out=pg[:], in_=pst[:].rearrange("p t c -> p c t"))
@@ -250,3 +269,7 @@ def tile_merge_mixtralsparsemoeblock_pa_l_kernel(tc, x, Wmean1, Wmean3, du1, dv1
                         if n + 1 < I_CHUNKS and t_next < first_block_of_chunk[n + 2]:
                             transpose_block(t_next)
                             t_next += 1
+                if m + 1 in RUN_AFTER:
+                    for rep in range(RUN_BLOCKS):
+                        if n + 1 < I_CHUNKS and t_next + rep < first_block_of_chunk[n + 2]:
+                            sort_block(t_next + rep)

@@ -22,14 +22,13 @@ H_PASSES = H // K_PASS
 R_PASSES = R // K_PASS
 TOKEN_CHUNKS = T // CHUNK
 TOKEN_TILES = T // P
-I_CHUNKS = (I + CHUNK - 1) // CHUNK
 
+CHUNK_WIDTHS = (512,) * 10 + (256,)
 RAW_BUFS = 8
-HEAD_BLOCKS = 15
-STAGE1_BLOCKS = {0: 3, 1: 3, 2: 3, 3: 3, 4: 3, 5: 3, 6: 3, 7: 3, 8: 3, 9: 3, 10: 3, 12: 4, 14: 4, 16: 4, 18: 4, 20: 4}
-RUN_AFTER = (1, 4, 7, 10, 13)
-RUN_BLOCKS = 4
-SORT_FROM = 48
+HEAD_SLOTS = 7
+STAGE1_SLOTS = 8 * TOKEN_CHUNKS
+FIRST_DVE_CHUNK = 1
+QUADRANT_ORDER = (0, 2, 1, 3)
 
 
 def tile_merge_mixtralsparsemoeblock_pa_l_kernel(tc, x, Wmean1, Wmean3, du1, dv1, du3, dv3, out):
@@ -37,11 +36,12 @@ def tile_merge_mixtralsparsemoeblock_pa_l_kernel(tc, x, Wmean1, Wmean3, du1, dv1
     with ExitStack() as ctx:
         keep = ctx.enter_context(tc.tile_pool(name="keep", bufs=1))
         rawp = ctx.enter_context(tc.tile_pool(name="rawp", bufs=RAW_BUFS))
-        grpp = ctx.enter_context(tc.tile_pool(name="grpp", bufs=8))
+        grpp = ctx.enter_context(tc.tile_pool(name="grpp", bufs=6))
         wcp = ctx.enter_context(tc.tile_pool(name="wcp", bufs=22))
         pstp = ctx.enter_context(tc.tile_pool(name="pstp", bufs=2))
         srtp = ctx.enter_context(tc.tile_pool(name="srtp", bufs=4))
-        epi = ctx.enter_context(tc.tile_pool(name="epi", bufs=4))
+        dvep = ctx.enter_context(tc.tile_pool(name="dvep", bufs=2))
+        epi = ctx.enter_context(tc.tile_pool(name="epi", bufs=3))
         tpp = ctx.enter_context(tc.psum_pool(name="tpp", bufs=4))
         accp = ctx.enter_context(tc.psum_pool(name="accp", bufs=4))
 
@@ -54,58 +54,95 @@ def tile_merge_mixtralsparsemoeblock_pa_l_kernel(tc, x, Wmean1, Wmean3, du1, dv1
 
         ctx.enter_context(tc.manual_schedule())
 
-        x_view = x.rearrange("(a j p) k -> a p j k", j=2, p=P)
-        w_view = (
-            Wmean1.rearrange("(a j p) k -> a p j k", j=2, p=P),
-            Wmean3.rearrange("(a j p) k -> a p j k", j=2, p=P),
-        )
-        du_view = (
-            du1.rearrange("(a j p) k -> a p j k", j=2, p=P),
-            du3.rearrange("(a j p) k -> a p j k", j=2, p=P),
-        )
+        def slabs(ap):
+            return ap.rearrange("(a j p) k -> a p j k", j=2, p=P)
+
+        def quadrants(ap):
+            return ap.rearrange("(a bb i) (q w) -> a q i bb w", bb=8, i=32, q=4)
+
+        x_view = slabs(x)
+        w_slabs = (slabs(Wmean1), slabs(Wmean3))
+        w_quads = (quadrants(Wmean1), quadrants(Wmean3))
+        du_view = (slabs(du1), slabs(du3))
         dv_view = (
             dv1.rearrange("(g m b j) k -> g b m j k", m=P, b=2, j=2),
             dv3.rearrange("(g m b j) k -> g b m j k", m=P, b=2, j=2),
         )
 
+        chunk_start = []
+        for ci in range(len(CHUNK_WIDTHS)):
+            chunk_start.append(sum(CHUNK_WIDTHS[:ci]))
+
         jobs = []
+        plan = {}
+
+        def push(stage, slot, item):
+            if (stage, slot) not in plan:
+                plan[(stage, slot)] = []
+            plan[(stage, slot)].append(item)
+
+        early = []
         for b in range(2):
-            jobs.append((x_view[b], H_PASSES, ("x", 0), b))
+            early.append((x_view[b], ("x", 0), b))
         for i in range(2):
             for gr in range(R_PASSES):
                 for b in range(2):
-                    jobs.append((dv_view[i][gr, b], H_PASSES, ("dv", i, gr), b))
+                    early.append((dv_view[i][gr, b], ("dv", i, gr), b))
         for c in range(1, TOKEN_CHUNKS):
             for b in range(2):
-                jobs.append((x_view[2 * c + b], H_PASSES, ("x", c), b))
-        for n in range(I_CHUNKS):
-            halves = min(CHUNK, I - n * CHUNK) // HALF
+                early.append((x_view[2 * c + b], ("x", c), b))
+        early_slots = (-7, -6, -5, -4, -3, -2, -1, 0, 1, 2, 3, 4, 7, 9, 13, 15)
+        for k in range(len(early)):
+            jobs.append((early[k][0], H_PASSES, early[k][1], early[k][2], "pe", (early_slots[k],) * H_PASSES))
+
+        for ci in range(len(CHUNK_WIDTHS)):
+            halves = CHUNK_WIDTHS[ci] // HALF
+            base = STAGE1_SLOTS + TOKEN_TILES * ci
+            a0 = chunk_start[ci] // HALF
+            count = 0
             for i in range(2):
                 for b in range(halves):
-                    jobs.append((w_view[i][2 * n + b], H_PASSES, ("w", n, i), b))
+                    if ci < FIRST_DVE_CHUNK:
+                        s0 = 17 + 2 * count
+                        jobs.append((w_slabs[i][a0 + b], H_PASSES, ("w", ci, i), b, "pe", (s0,) * H_PASSES))
+                    else:
+                        s0 = base - 16 + 3 * count
+                        jobs.append((w_quads[i][a0 + b], H_PASSES, ("w", ci, i), b, "dve", (s0, s0 + 1, s0 + 2)))
+                    count += 1
             for i in range(2):
                 for b in range(halves):
-                    jobs.append((du_view[i][2 * n + b], R_PASSES, ("du", n, i), b))
+                    if ci < FIRST_DVE_CHUNK:
+                        s0 = 25 + 2 * i
+                    else:
+                        s0 = base - 5 + 2 * i
+                    jobs.append((du_view[i][a0 + b], R_PASSES, ("du", ci, i), b, "pe", (s0,) * R_PASSES))
 
         blocks = []
-        loads_after = {}
+        last_use = {}
         for jb in range(len(jobs)):
             for g in range(jobs[jb][1]):
+                bi = len(blocks)
                 blocks.append((jb, g))
-            if jb + RAW_BUFS < len(jobs):
-                loads_after[len(blocks) - 1] = jb + RAW_BUFS
-
-        first_block_of_chunk = {}
-        for bi in range(len(blocks)):
-            key = jobs[blocks[bi][0]][2]
-            if key[0] == "w" and key[1] not in first_block_of_chunk:
-                first_block_of_chunk[key[1]] = bi
-        first_block_of_chunk[I_CHUNKS] = len(blocks)
+                s0 = jobs[jb][5][g]
+                if jobs[jb][4] == "pe":
+                    push("sort", s0, bi)
+                    push("T", s0, bi)
+                    push("Q", s0 + 1, bi)
+                else:
+                    push("S", s0, bi)
+                    push("V", s0 + 1, bi)
+                    push("I", s0 + 2, bi)
+                    push("Q", s0 + 3, bi)
+                last_use[jb] = bi
 
         raw_of = {}
-        grp_of = {}
         srt_of = {}
+        s1_of = {}
+        v1_of = {}
+        grp_of = {}
         units = {}
+        done = {}
+        next_load = [0]
 
         def unit_tiles(key, g):
             if (key, g) not in units:
@@ -119,43 +156,70 @@ def tile_merge_mixtralsparsemoeblock_pa_l_kernel(tc, x, Wmean1, Wmean3, du1, dv1
                 units[(key, g)] = (codes, scales)
             return units[(key, g)]
 
-        def load(jb):
-            raw = rawp.tile([P, 2, jobs[jb][1] * K_PASS], BF16, name="raw", tag="raw")
-            nc.sync.dma_start(out=raw[:], in_=jobs[jb][0])
-            raw_of[jb] = raw
+        def issue_loads():
+            while next_load[0] < len(jobs) and (next_load[0] < RAW_BUFS or (next_load[0] - RAW_BUFS) in done):
+                jb = next_load[0]
+                width = jobs[jb][1] * K_PASS
+                if jobs[jb][4] == "pe":
+                    raw = rawp.tile([P, 2, width], BF16, name="raw", tag="raw")
+                    nc.sync.dma_start(out=raw[:], in_=jobs[jb][0])
+                else:
+                    raw = rawp.tile([P, 8, width // 4], BF16, name="raw", tag="raw")
+                    for q in QUADRANT_ORDER:
+                        nc.sync.dma_start(out=raw[32 * q : 32 * (q + 1), :, :], in_=jobs[jb][0][q])
+                raw_of[jb] = raw
+                next_load[0] = jb + 1
+
+        def consumed(bi):
+            if last_use[blocks[bi][0]] == bi:
+                done[blocks[bi][0]] = True
 
         def sort_block(bi):
-            if bi < SORT_FROM or bi >= len(blocks):
-                return
             jb, g = blocks[bi]
             words = raw_of[jb][:].bitcast(F32)
             srt = srtp.tile([P, 2, 2, P], F32, name="srt", tag="srt")
-            nc.vector.tensor_copy(
-                out=srt[:], in_=words[:, :, 256 * g : 256 * (g + 1)].rearrange("p j (q u) -> p j u q", u=2)
-            )
+            if jobs[jb][1] == H_PASSES:
+                for j in range(2):
+                    nc.vector.tensor_copy(
+                        out=srt[:, j, :, :].rearrange("p u (q jj) -> p u q jj", q=4),
+                        in_=words[:, j, :].rearrange("p (q g jj u) -> p g u q jj", q=4, g=H_PASSES, u=2)[:, g],
+                    )
+            else:
+                nc.vector.tensor_copy(
+                    out=srt[:], in_=words[:, :, 256 * g : 256 * (g + 1)].rearrange("p j (q u) -> p j u q", u=2)
+                )
             srt_of[bi] = srt
+            consumed(bi)
 
         def transpose_block(bi):
-            jb, g = blocks[bi]
-            words = raw_of[jb][:].bitcast(F32)
             tp = tpp.tile([P, 2, 2, P], F32, name="tp", tag="tp")
             for j in range(2):
                 for u in range(2):
-                    if bi in srt_of:
-                        nc.tensor.transpose(tp[:, j, u, :], srt_of[bi][:, j, u, :], ident[:])
-                    else:
-                        nc.tensor.transpose(tp[:, j, u, :], words[:, j, 256 * g + u : 256 * (g + 1) : 2], ident[:])
+                    nc.tensor.transpose(tp[:, j, u, :], srt_of[bi][:, j, u, :], ident[:])
             grp = grpp.tile([P, HALF, 4], BF16, name="grp", tag="grp", align_bytes=64)
-            dst = grp[:].bitcast(F32).rearrange("p (j r) u -> p j r u", j=2)
-            src = tp[:].rearrange("p j u r -> p j r u")
-            on_scalar = (bi % 3 != 2) if bi < first_block_of_chunk[0] else True
-            if on_scalar:
-                nc.scalar.copy(out=dst, in_=src)
-            else:
-                nc.vector.tensor_copy(out=dst, in_=src)
+            nc.scalar.copy(
+                out=grp[:].bitcast(F32).rearrange("p (j r) u -> p j r u", j=2),
+                in_=tp[:].rearrange("p j u r -> p j r u"),
+            )
             grp_of[bi] = grp
-            if bi in loads_after:
-                load(loads_after[bi])
+
+        def presort_block(bi):
+            jb, g = blocks[bi]
+            words = raw_of[jb][:].bitcast(F32)
+            s1 = dvep.tile([P, 2, 8, 32], F32, name="s1", tag="s1", align_bytes=64)
+            nc.scalar.copy(out=s1[:], in_=words[:, :, 64 * g : 64 * (g + 1)].rearrange("p bb (j u) -> p u bb j", u=2))
+            s1_of[bi] = s1
+            consumed(bi)
+
+        def vector_transpose_block(bi):
+            v1 = dvep.tile([P, 2 * HALF], F32, name="v1", tag="v1", align_bytes=64)
+            nc.vector.transpose(out=v1[:], in_=s1_of[bi][:].rearrange("p u bb j -> p (u bb j)"))
+            v1_of[bi] = v1
+
+        def interleave_block(bi):
+            grp = grpp.tile([P, HALF, 4], BF16, name="grp", tag="grp", align_bytes=64)
+            nc.vector.tensor_copy(out=grp[:].bitcast(F32), in_=v1_of[bi][:].rearrange("p (u r) -> p r u", u=2))
+            grp_of[bi] = grp
 
         def quantize_block(bi):
             jb, g = blocks[bi]
@@ -185,17 +249,17 @@ def tile_merge_mixtralsparsemoeblock_pa_l_kernel(tc, x, Wmean1, Wmean3, du1, dv1
                     )
                 nc.scalar.copy(out=pst[:, t, :], in_=acc[:])
 
-        def output_tile(n, m):
-            width = min(CHUNK, I - n * CHUNK)
+        def output_tile(ci, m):
+            width = CHUNK_WIDTHS[ci]
             c = m // 4
             tok = slice(P * (m % 4), P * (m % 4 + 1))
             banks = []
             for i in range(2):
                 pairs = []
                 for g in range(H_PASSES):
-                    pairs.append((units[(("x", c), g)], units[(("w", n, i), g)]))
+                    pairs.append((units[(("x", c), g)], units[(("w", ci, i), g)]))
                 for gr in range(R_PASSES):
-                    pairs.append((units[(("p", i, gr), c)], units[(("du", n, i), gr)]))
+                    pairs.append((units[(("p", i, gr), c)], units[(("du", ci, i), gr)]))
                 acc = accp.tile([P, CHUNK], F32, name="acc", tag="acc")
                 for q in range(len(pairs)):
                     (ac, asc), (wc, wsc) = pairs[q]
@@ -213,63 +277,49 @@ def tile_merge_mixtralsparsemoeblock_pa_l_kernel(tc, x, Wmean1, Wmean3, du1, dv1
             nc.scalar.activation(out=sg[:, :width], in_=banks[0][:, :width], func=SILU)
             z = epi.tile([P, CHUNK], F32, name="z", tag="z")
             nc.vector.tensor_tensor(out=z[:, :width], in0=banks[1][:, :width], in1=sg[:, :width], op=MULT)
-            nc.sync.dma_start(out=out[P * m : P * (m + 1), CHUNK * n : CHUNK * n + width], in_=z[:, :width])
+            first = chunk_start[ci]
+            nc.sync.dma_start(out=out[P * m : P * (m + 1), first : first + width], in_=z[:, :width])
 
-        for jb in range(RAW_BUFS):
-            load(jb)
-        t_next = 0
-        q_next = 0
-        for rep in range(HEAD_BLOCKS):
-            transpose_block(t_next)
-            t_next += 1
-            if t_next - q_next > 2:
-                quantize_block(q_next)
-                q_next += 1
-
+        issue_loads()
         waiting_p = []
         pst = None
-        for k in range(2 * 4 * TOKEN_CHUNKS):
-            c = k // 8
-            i = (k % 8) // 4
-            gr = ((k % 8) // 2) % 2
-            h = k % 2
-            while q_next < t_next:
-                quantize_block(q_next)
-                q_next += 1
-            if h == 0:
-                pst = pstp.tile([P, 4, CHUNK], BF16, name="pst", tag="pst")
-            p_groups(i, gr, c, h, pst)
-            for item in waiting_p:
-                pc, psc = unit_tiles(item[1], item[2])
-                nc.vector.quantize_mx(
-                    out=pc[:].bitcast(FP8X4), scales=psc[:], in_=item[0][:].rearrange("p c t -> p (c t)")
-                )
-            waiting_p = []
-            for rep in range(STAGE1_BLOCKS.get(k + 1, 0)):
-                sort_block(t_next + STAGE1_BLOCKS.get(k, 0) + rep)
-            if h == 1:
-                pg = pstp.tile([P, CHUNK, 4], BF16, name="pg", tag="pg", align_bytes=64)
-                nc.vector.tensor_copy(out=pg[:], in_=pst[:].rearrange("p t c -> p c t"))
-                waiting_p.append((pg, ("p", i, gr), c))
-            for rep in range(STAGE1_BLOCKS.get(k, 0)):
-                transpose_block(t_next)
-                t_next += 1
-        for item in waiting_p:
-            pc, psc = unit_tiles(item[1], item[2])
-            nc.vector.quantize_mx(out=pc[:].bitcast(FP8X4), scales=psc[:], in_=item[0][:].rearrange("p c t -> p (c t)"))
-
-        for n in range(I_CHUNKS):
-            for m in range(TOKEN_TILES):
-                output_tile(n, m)
-                while q_next < t_next:
-                    quantize_block(q_next)
-                    q_next += 1
-                if m in RUN_AFTER:
-                    for rep in range(RUN_BLOCKS):
-                        if n + 1 < I_CHUNKS and t_next < first_block_of_chunk[n + 2]:
-                            transpose_block(t_next)
-                            t_next += 1
-                if m + 1 in RUN_AFTER:
-                    for rep in range(RUN_BLOCKS):
-                        if n + 1 < I_CHUNKS and t_next + rep < first_block_of_chunk[n + 2]:
-                            sort_block(t_next + rep)
+        for s in range(-HEAD_SLOTS, STAGE1_SLOTS + TOKEN_TILES * len(CHUNK_WIDTHS)):
+            for bi in plan.get(("V", s), []):
+                vector_transpose_block(bi)
+            for bi in plan.get(("I", s), []):
+                interleave_block(bi)
+            for bi in plan.get(("sort", s), []):
+                sort_block(bi)
+            for bi in plan.get(("S", s), []):
+                presort_block(bi)
+            if 0 <= s < STAGE1_SLOTS:
+                c = s // 8
+                i = (s % 8) // 4
+                gr = ((s % 8) // 2) % 2
+                h = s % 2
+                if h == 0:
+                    pst = pstp.tile([P, 4, CHUNK], BF16, name="pst", tag="pst")
+                p_groups(i, gr, c, h, pst)
+                for item in waiting_p:
+                    pc, psc = unit_tiles(item[1], item[2])
+                    nc.vector.quantize_mx(
+                        out=pc[:].bitcast(FP8X4), scales=psc[:], in_=item[0][:].rearrange("p c t -> p (c t)")
+                    )
+                waiting_p = []
+                if h == 1:
+                    pg = pstp.tile([P, CHUNK, 4], BF16, name="pg", tag="pg", align_bytes=64)
+                    nc.vector.tensor_copy(out=pg[:], in_=pst[:].rearrange("p t c -> p c t"))
+                    waiting_p.append((pg, ("p", i, gr), c))
+            elif s >= STAGE1_SLOTS:
+                for item in waiting_p:
+                    pc, psc = unit_tiles(item[1], item[2])
+                    nc.vector.quantize_mx(
+                        out=pc[:].bitcast(FP8X4), scales=psc[:], in_=item[0][:].rearrange("p c t -> p (c t)")
+                    )
+                waiting_p = []
+                output_tile((s - STAGE1_SLOTS) // TOKEN_TILES, (s - STAGE1_SLOTS) % TOKEN_TILES)
+            for bi in plan.get(("Q", s), []):
+                quantize_block(bi)
+            for bi in plan.get(("T", s), []):
+                transpose_block(bi)
+            issue_loads()

@@ -24,11 +24,19 @@ TOKEN_CHUNKS = T // CHUNK
 TOKEN_TILES = T // P
 
 CHUNK_WIDTHS = (512,) * 10 + (256,)
-RAW_BUFS = 8
-HEAD_SLOTS = 7
+RAW_BUFS = 3
+HEAD_SLOTS = 5
 STAGE1_SLOTS = 8 * TOKEN_CHUNKS
 FIRST_DVE_CHUNK = 1
-QUADRANT_ORDER = (0, 2, 1, 3)
+TWO_QUEUES = True
+INTERLEAVE_ON_SCALAR_EVERY = 2
+EARLY_SLOTS = (-5, -4, -3, -2, -1, 0, 1, 2, 3, 4, 5, 6, 8, 10, 13, 15)
+CHUNK0_SLOTS = (17, 19, 21, 23, 25, 26, 27, 28)
+UNIT_SPAN = 15
+UNIT_LEAD = 19
+NARROW_P = False
+LOADS_PER_SLOT = 1
+SORT_ON_SCALAR_EVERY = 1000
 
 
 def tile_merge_mixtralsparsemoeblock_pa_l_kernel(tc, x, Wmean1, Wmean3, du1, dv1, du3, dv3, out):
@@ -39,9 +47,8 @@ def tile_merge_mixtralsparsemoeblock_pa_l_kernel(tc, x, Wmean1, Wmean3, du1, dv1
         grpp = ctx.enter_context(tc.tile_pool(name="grpp", bufs=6))
         wcp = ctx.enter_context(tc.tile_pool(name="wcp", bufs=22))
         pstp = ctx.enter_context(tc.tile_pool(name="pstp", bufs=2))
-        srtp = ctx.enter_context(tc.tile_pool(name="srtp", bufs=4))
-        dvep = ctx.enter_context(tc.tile_pool(name="dvep", bufs=2))
-        epi = ctx.enter_context(tc.tile_pool(name="epi", bufs=3))
+        stgp = ctx.enter_context(tc.tile_pool(name="stgp", bufs=3))
+        epi = ctx.enter_context(tc.tile_pool(name="epi", bufs=7))
         tpp = ctx.enter_context(tc.psum_pool(name="tpp", bufs=4))
         accp = ctx.enter_context(tc.psum_pool(name="accp", bufs=4))
 
@@ -54,95 +61,112 @@ def tile_merge_mixtralsparsemoeblock_pa_l_kernel(tc, x, Wmean1, Wmean3, du1, dv1
 
         ctx.enter_context(tc.manual_schedule())
 
-        def slabs(ap):
-            return ap.rearrange("(a j p) k -> a p j k", j=2, p=P)
-
-        def quadrants(ap):
-            return ap.rearrange("(a bb i) (q w) -> a q i bb w", bb=8, i=32, q=4)
-
-        x_view = slabs(x)
-        w_slabs = (slabs(Wmean1), slabs(Wmean3))
-        w_quads = (quadrants(Wmean1), quadrants(Wmean3))
-        du_view = (slabs(du1), slabs(du3))
-        dv_view = (
-            dv1.rearrange("(g m b j) k -> g b m j k", m=P, b=2, j=2),
-            dv3.rearrange("(g m b j) k -> g b m j k", m=P, b=2, j=2),
-        )
+        weights = {"w": (Wmean1, Wmean3), "du": (du1, du3)}
+        dv_in = (dv1, dv3)
 
         chunk_start = []
         for ci in range(len(CHUNK_WIDTHS)):
             chunk_start.append(sum(CHUNK_WIDTHS[:ci]))
 
         jobs = []
+        blocks = []
         plan = {}
+        uses_left = {}
 
         def push(stage, slot, item):
             if (stage, slot) not in plan:
                 plan[(stage, slot)] = []
             plan[(stage, slot)].append(item)
 
-        early = []
-        for b in range(2):
-            early.append((x_view[b], ("x", 0), b))
+        def add_tensor_job(sources, passes, key, slots):
+            jb = len(jobs)
+            jobs.append((sources, passes, key, "pe", HALF * len(sources)))
+            uses_left[jb] = [passes * len(sources)]
+            for b in range(len(sources)):
+                for g in range(passes):
+                    bi = len(blocks)
+                    blocks.append((jb, b, g))
+                    push("sort", slots[b], bi)
+                    push("T", slots[b], bi)
+                    if key[0] != "dv":
+                        push("Q", slots[b] + 1, bi)
+                    elif b == 1:
+                        push("Qwide", slots[b] + 1, (key, g))
+
+        def add_vector_job(sources, passes, key, rows, slots):
+            jb = len(jobs)
+            jobs.append((sources, passes, key, "dve", rows))
+            uses_left[jb] = [passes]
+            for g in range(passes):
+                bi = len(blocks)
+                blocks.append((jb, 0, g))
+                push("S", slots[g], bi)
+                push("V", slots[g] + 1, bi)
+                push("I", slots[g] + 2, bi)
+                push("Q", slots[g] + 3, bi)
+
+        def slabs(ap):
+            return ap.rearrange("(b j p) k -> b p j k", j=2, p=P)
+
+        def dv_slabs(ap, gr):
+            return ap.rearrange("(b j g r) k -> g b r j k", b=2, j=2, g=R_PASSES)[gr]
+
+        def halves_of(view, n):
+            parts = []
+            for b in range(n):
+                parts.append(view[b])
+            return parts
+
+        def quadrants_of(ap):
+            view = ap.rearrange("(bb i) (q w) -> q i bb w", i=32, q=4)
+            return halves_of(view, 4)
+
+        add_tensor_job(halves_of(slabs(x[0:CHUNK, :]), 2), H_PASSES, ("x", 0), EARLY_SLOTS[0:2])
         for i in range(2):
             for gr in range(R_PASSES):
-                for b in range(2):
-                    early.append((dv_view[i][gr, b], ("dv", i, gr), b))
+                k = 2 + 4 * i + 2 * gr
+                add_tensor_job(halves_of(dv_slabs(dv_in[i], gr), 2), H_PASSES, ("dv", i, gr), EARLY_SLOTS[k : k + 2])
         for c in range(1, TOKEN_CHUNKS):
-            for b in range(2):
-                early.append((x_view[2 * c + b], ("x", c), b))
-        early_slots = (-7, -6, -5, -4, -3, -2, -1, 0, 1, 2, 3, 4, 7, 9, 13, 15)
-        for k in range(len(early)):
-            jobs.append((early[k][0], H_PASSES, early[k][1], early[k][2], "pe", (early_slots[k],) * H_PASSES))
+            add_tensor_job(
+                halves_of(slabs(x[CHUNK * c : CHUNK * (c + 1), :]), 2),
+                H_PASSES,
+                ("x", c),
+                EARLY_SLOTS[8 + 2 * c : 10 + 2 * c],
+            )
 
         for ci in range(len(CHUNK_WIDTHS)):
-            halves = CHUNK_WIDTHS[ci] // HALF
+            width = CHUNK_WIDTHS[ci]
             base = STAGE1_SLOTS + TOKEN_TILES * ci
-            a0 = chunk_start[ci] // HALF
+            seen = 0
             count = 0
-            for i in range(2):
-                for b in range(halves):
+            for kind in ("w", "du"):
+                passes = H_PASSES if kind == "w" else R_PASSES
+                for i in range(2):
+                    rows = weights[kind][i][chunk_start[ci] : chunk_start[ci] + width, :]
                     if ci < FIRST_DVE_CHUNK:
-                        s0 = 17 + 2 * count
-                        jobs.append((w_slabs[i][a0 + b], H_PASSES, ("w", ci, i), b, "pe", (s0,) * H_PASSES))
+                        add_tensor_job(
+                            halves_of(slabs(rows), width // HALF),
+                            passes,
+                            (kind, ci, i),
+                            CHUNK0_SLOTS[2 * count : 2 * count + 2],
+                        )
                     else:
-                        s0 = base - 16 + 3 * count
-                        jobs.append((w_quads[i][a0 + b], H_PASSES, ("w", ci, i), b, "dve", (s0, s0 + 1, s0 + 2)))
+                        slots = []
+                        for g in range(passes):
+                            slots.append(base - UNIT_LEAD + (UNIT_SPAN * seen) // (2 * (H_PASSES + R_PASSES)))
+                            seen += 1
+                        add_vector_job(quadrants_of(rows), passes, (kind, ci, i), width, slots)
                     count += 1
-            for i in range(2):
-                for b in range(halves):
-                    if ci < FIRST_DVE_CHUNK:
-                        s0 = 25 + 2 * i
-                    else:
-                        s0 = base - 5 + 2 * i
-                    jobs.append((du_view[i][a0 + b], R_PASSES, ("du", ci, i), b, "pe", (s0,) * R_PASSES))
-
-        blocks = []
-        last_use = {}
-        for jb in range(len(jobs)):
-            for g in range(jobs[jb][1]):
-                bi = len(blocks)
-                blocks.append((jb, g))
-                s0 = jobs[jb][5][g]
-                if jobs[jb][4] == "pe":
-                    push("sort", s0, bi)
-                    push("T", s0, bi)
-                    push("Q", s0 + 1, bi)
-                else:
-                    push("S", s0, bi)
-                    push("V", s0 + 1, bi)
-                    push("I", s0 + 2, bi)
-                    push("Q", s0 + 3, bi)
-                last_use[jb] = bi
 
         raw_of = {}
-        srt_of = {}
-        s1_of = {}
+        stg_of = {}
         v1_of = {}
         grp_of = {}
+        wide_of = {}
         units = {}
         done = {}
         next_load = [0]
+        waiting_loads = [[], []]
 
         def unit_tiles(key, g):
             if (key, g) not in units:
@@ -156,79 +180,106 @@ def tile_merge_mixtralsparsemoeblock_pa_l_kernel(tc, x, Wmean1, Wmean3, du1, dv1
                 units[(key, g)] = (codes, scales)
             return units[(key, g)]
 
-        def issue_loads():
+        def issue_loads(limit):
             while next_load[0] < len(jobs) and (next_load[0] < RAW_BUFS or (next_load[0] - RAW_BUFS) in done):
                 jb = next_load[0]
-                width = jobs[jb][1] * K_PASS
-                if jobs[jb][4] == "pe":
-                    raw = rawp.tile([P, 2, width], BF16, name="raw", tag="raw")
-                    nc.sync.dma_start(out=raw[:], in_=jobs[jb][0])
+                sources, passes, key, path, rows = jobs[jb]
+                if path == "pe":
+                    raw = rawp.tile([P, rows // P, passes * K_PASS], BF16, name="raw", tag="raw")
+                    for b in range(len(sources)):
+                        waiting_loads[0].append((raw[:, 2 * b : 2 * b + 2, :], sources[b]))
                 else:
-                    raw = rawp.tile([P, 8, width // 4], BF16, name="raw", tag="raw")
-                    for q in QUADRANT_ORDER:
-                        nc.sync.dma_start(out=raw[32 * q : 32 * (q + 1), :, :], in_=jobs[jb][0][q])
+                    raw = rawp.tile([P, rows // 32, passes * K_PASS // 4], BF16, name="raw", tag="raw")
+                    for q in (0, 2, 1, 3):
+                        lane = 1 if (TWO_QUEUES and q >= 2) else 0
+                        waiting_loads[lane].append((raw[32 * q : 32 * (q + 1), :, :], sources[q]))
                 raw_of[jb] = raw
                 next_load[0] = jb + 1
+            for lane in range(2):
+                queue = nc.scalar if lane == 1 else nc.sync
+                for item in waiting_loads[lane][:limit]:
+                    queue.dma_start(out=item[0], in_=item[1])
+                waiting_loads[lane] = waiting_loads[lane][limit:]
 
-        def consumed(bi):
-            if last_use[blocks[bi][0]] == bi:
-                done[blocks[bi][0]] = True
+        def consumed(jb):
+            uses_left[jb][0] -= 1
+            if uses_left[jb][0] == 0:
+                done[jb] = True
 
         def sort_block(bi):
-            jb, g = blocks[bi]
+            jb, b, g = blocks[bi]
             words = raw_of[jb][:].bitcast(F32)
-            srt = srtp.tile([P, 2, 2, P], F32, name="srt", tag="srt")
-            if jobs[jb][1] == H_PASSES:
-                for j in range(2):
-                    nc.vector.tensor_copy(
-                        out=srt[:, j, :, :].rearrange("p u (q jj) -> p u q jj", q=4),
-                        in_=words[:, j, :].rearrange("p (q g jj u) -> p g u q jj", q=4, g=H_PASSES, u=2)[:, g],
-                    )
-            else:
-                nc.vector.tensor_copy(
-                    out=srt[:], in_=words[:, :, 256 * g : 256 * (g + 1)].rearrange("p j (q u) -> p j u q", u=2)
-                )
-            srt_of[bi] = srt
-            consumed(bi)
+            srt = epi.tile([P, 2, 2, P], F32, name="srt", tag="w2k")
+            for j in range(2):
+                dst = srt[:, j, :, :].rearrange("p u (q jj) -> p u q jj", q=4)
+                src = words[:, 2 * b + j, :].rearrange("p (q g jj u) -> p g u q jj", q=4, g=jobs[jb][1], u=2)[:, g]
+                if bi % SORT_ON_SCALAR_EVERY == 0:
+                    nc.scalar.copy(out=dst, in_=src)
+                else:
+                    nc.vector.tensor_copy(out=dst, in_=src)
+            stg_of[bi] = srt
+            consumed(jb)
 
         def transpose_block(bi):
+            jb, b, g = blocks[bi]
+            key = jobs[jb][2]
             tp = tpp.tile([P, 2, 2, P], F32, name="tp", tag="tp")
             for j in range(2):
                 for u in range(2):
-                    nc.tensor.transpose(tp[:, j, u, :], srt_of[bi][:, j, u, :], ident[:])
-            grp = grpp.tile([P, HALF, 4], BF16, name="grp", tag="grp", align_bytes=64)
-            nc.scalar.copy(
-                out=grp[:].bitcast(F32).rearrange("p (j r) u -> p j r u", j=2),
-                in_=tp[:].rearrange("p j u r -> p j r u"),
-            )
-            grp_of[bi] = grp
+                    nc.tensor.transpose(tp[:, j, u, :], stg_of[bi][:, j, u, :], ident[:])
+            if key[0] == "dv":
+                if (key, g) not in wide_of:
+                    wide_of[(key, g)] = grpp.tile([P, CHUNK, 4], BF16, name="gdv", tag="grp", align_bytes=64)
+                view = wide_of[(key, g)][:].bitcast(F32).rearrange("p (t qq jj) u -> p t qq jj u", t=4, qq=4)
+                for j in range(2):
+                    nc.scalar.copy(
+                        out=view[:, :, 2 * b + j, :, :],
+                        in_=tp[:, j, :, :].rearrange("p u (jj t) -> p t jj u", t=4),
+                    )
+            else:
+                grp = grpp.tile([P, HALF, 4], BF16, name="grp", tag="grp", align_bytes=64)
+                nc.scalar.copy(
+                    out=grp[:].bitcast(F32).rearrange("p (j r) u -> p j r u", j=2),
+                    in_=tp[:].rearrange("p j u r -> p j r u"),
+                )
+                grp_of[bi] = grp
 
-        def presort_block(bi):
-            jb, g = blocks[bi]
+        def presort_unit(bi):
+            jb, b, g = blocks[bi]
             words = raw_of[jb][:].bitcast(F32)
-            s1 = dvep.tile([P, 2, 8, 32], F32, name="s1", tag="s1", align_bytes=64)
+            s1 = stgp.tile([P, 2, jobs[jb][4] // 32, 32], F32, name="s1", tag="s1", align_bytes=64)
             nc.scalar.copy(out=s1[:], in_=words[:, :, 64 * g : 64 * (g + 1)].rearrange("p bb (j u) -> p u bb j", u=2))
-            s1_of[bi] = s1
-            consumed(bi)
+            stg_of[bi] = s1
+            consumed(jb)
 
-        def vector_transpose_block(bi):
-            v1 = dvep.tile([P, 2 * HALF], F32, name="v1", tag="v1", align_bytes=64)
-            nc.vector.transpose(out=v1[:], in_=s1_of[bi][:].rearrange("p u bb j -> p (u bb j)"))
+        def vector_transpose_unit(bi):
+            v1 = stgp.tile([P, 2 * jobs[blocks[bi][0]][4]], F32, name="v1", tag="v1", bufs=2, align_bytes=64)
+            nc.vector.transpose(out=v1[:], in_=stg_of[bi][:].rearrange("p u bb j -> p (u bb j)"))
             v1_of[bi] = v1
 
-        def interleave_block(bi):
-            grp = grpp.tile([P, HALF, 4], BF16, name="grp", tag="grp", align_bytes=64)
-            nc.vector.tensor_copy(out=grp[:].bitcast(F32), in_=v1_of[bi][:].rearrange("p (u r) -> p r u", u=2))
+        def interleave_unit(bi):
+            grp = grpp.tile([P, jobs[blocks[bi][0]][4], 4], BF16, name="grp", tag="grp", align_bytes=64)
+            if bi % INTERLEAVE_ON_SCALAR_EVERY == 0:
+                nc.scalar.copy(out=grp[:].bitcast(F32), in_=v1_of[bi][:].rearrange("p (u r) -> p r u", u=2))
+            else:
+                nc.vector.tensor_copy(out=grp[:].bitcast(F32), in_=v1_of[bi][:].rearrange("p (u r) -> p r u", u=2))
             grp_of[bi] = grp
 
         def quantize_block(bi):
-            jb, g = blocks[bi]
+            jb, b, g = blocks[bi]
             codes, scales = unit_tiles(jobs[jb][2], g)
-            cols = slice(HALF * jobs[jb][3], HALF * (jobs[jb][3] + 1))
+            n = HALF if jobs[jb][3] == "pe" else jobs[jb][4]
+            cols = slice(n * b, n * (b + 1))
             nc.vector.quantize_mx(
                 out=codes[:, cols].bitcast(FP8X4),
                 scales=scales[:, cols],
                 in_=grp_of[bi][:].rearrange("p r t -> p (r t)"),
+            )
+
+        def quantize_wide(tile_ap, key, g):
+            codes, scales = unit_tiles(key, g)
+            nc.vector.quantize_mx(
+                out=codes[:].bitcast(FP8X4), scales=scales[:], in_=tile_ap[:].rearrange("p c t -> p (c t)")
             )
 
         def p_groups(i, gr, c, h, pst):
@@ -248,6 +299,26 @@ def tile_merge_mixtralsparsemoeblock_pa_l_kernel(tc, x, Wmean1, Wmean3, du1, dv1
                         stop=(g == H_PASSES - 1),
                     )
                 nc.scalar.copy(out=pst[:, t, :], in_=acc[:])
+
+        def p_banks(i, gr, c, h, pg):
+            for tq in (2 * h, 2 * h + 1):
+                tok = slice(P * tq, P * (tq + 1))
+                acc = accp.tile([P, 4, P], F32, name="acc", tag="acc")
+                for t in range(4):
+                    cols = slice(P * t, P * (t + 1))
+                    for g in range(H_PASSES):
+                        dc, ds = units[(("dv", i, gr), g)]
+                        xc, xs = units[(("x", c), g)]
+                        nc.tensor.matmul_mx(
+                            out=acc[:, t, :],
+                            lhsT=dc[:, cols].bitcast(FP8X4),
+                            lhsT_scale=ds[:, cols],
+                            rhs=xc[:, tok].bitcast(FP8X4),
+                            rhs_scale=xs[:, tok],
+                            start=(g == 0),
+                            stop=(g == H_PASSES - 1),
+                        )
+                nc.scalar.copy(out=pg[:, tok, :], in_=acc[:].rearrange("p t c -> p c t"))
 
         def output_tile(ci, m):
             width = CHUNK_WIDTHS[ci]
@@ -273,53 +344,60 @@ def tile_merge_mixtralsparsemoeblock_pa_l_kernel(tc, x, Wmean1, Wmean3, du1, dv1
                         stop=(q == len(pairs) - 1),
                     )
                 banks.append(acc)
-            sg = epi.tile([P, CHUNK], F32, name="sg", tag="sg")
+            sg = epi.tile([P, CHUNK], F32, name="sg", tag="w2k")
             nc.scalar.activation(out=sg[:, :width], in_=banks[0][:, :width], func=SILU)
-            z = epi.tile([P, CHUNK], F32, name="z", tag="z")
+            z = epi.tile([P, CHUNK], F32, name="z", tag="w2k")
             nc.vector.tensor_tensor(out=z[:, :width], in0=banks[1][:, :width], in1=sg[:, :width], op=MULT)
             first = chunk_start[ci]
             nc.sync.dma_start(out=out[P * m : P * (m + 1), first : first + width], in_=z[:, :width])
 
-        issue_loads()
+        issue_loads(2 * RAW_BUFS)
         waiting_p = []
+        full_p = []
+        late_p = []
         pst = None
         for s in range(-HEAD_SLOTS, STAGE1_SLOTS + TOKEN_TILES * len(CHUNK_WIDTHS)):
             for bi in plan.get(("V", s), []):
-                vector_transpose_block(bi)
+                vector_transpose_unit(bi)
             for bi in plan.get(("I", s), []):
-                interleave_block(bi)
+                interleave_unit(bi)
             for bi in plan.get(("sort", s), []):
                 sort_block(bi)
             for bi in plan.get(("S", s), []):
-                presort_block(bi)
+                presort_unit(bi)
             if 0 <= s < STAGE1_SLOTS:
                 c = s // 8
                 i = (s % 8) // 4
                 gr = ((s % 8) // 2) % 2
                 h = s % 2
-                if h == 0:
-                    pst = pstp.tile([P, 4, CHUNK], BF16, name="pst", tag="pst")
-                p_groups(i, gr, c, h, pst)
-                for item in waiting_p:
-                    pc, psc = unit_tiles(item[1], item[2])
-                    nc.vector.quantize_mx(
-                        out=pc[:].bitcast(FP8X4), scales=psc[:], in_=item[0][:].rearrange("p c t -> p (c t)")
-                    )
-                waiting_p = []
-                if h == 1:
-                    pg = pstp.tile([P, CHUNK, 4], BF16, name="pg", tag="pg", align_bytes=64)
-                    nc.vector.tensor_copy(out=pg[:], in_=pst[:].rearrange("p t c -> p c t"))
-                    waiting_p.append((pg, ("p", i, gr), c))
+                if NARROW_P:
+                    if h == 0:
+                        pst = pstp.tile([P, CHUNK, 4], BF16, name="pg", tag="pg", align_bytes=64)
+                    p_banks(i, gr, c, h, pst)
+                    if h == 1:
+                        late_p.append((pst, ("p", i, gr), c))
+                else:
+                    if h == 0:
+                        pst = pstp.tile([P, 4, CHUNK], BF16, name="pst", tag="pst")
+                    p_groups(i, gr, c, h, pst)
+                    if h == 1:
+                        full_p.append((pst, ("p", i, gr), c))
             elif s >= STAGE1_SLOTS:
-                for item in waiting_p:
-                    pc, psc = unit_tiles(item[1], item[2])
-                    nc.vector.quantize_mx(
-                        out=pc[:].bitcast(FP8X4), scales=psc[:], in_=item[0][:].rearrange("p c t -> p (c t)")
-                    )
-                waiting_p = []
                 output_tile((s - STAGE1_SLOTS) // TOKEN_TILES, (s - STAGE1_SLOTS) % TOKEN_TILES)
             for bi in plan.get(("Q", s), []):
                 quantize_block(bi)
+            for item in plan.get(("Qwide", s), []):
+                quantize_wide(wide_of[item], item[0], item[1])
+            for item in waiting_p:
+                quantize_wide(item[0], item[1], item[2])
+            waiting_p = late_p
+            late_p = []
+            if len(full_p) > 0 and (s % 2 == 0 or s >= STAGE1_SLOTS):
+                item = full_p[0]
+                full_p = []
+                pg = pstp.tile([P, CHUNK, 4], BF16, name="pg", tag="pg", bufs=1, align_bytes=64)
+                nc.vector.tensor_copy(out=pg[:], in_=item[0][:].rearrange("p t c -> p c t"))
+                waiting_p.append((pg, item[1], item[2]))
             for bi in plan.get(("T", s), []):
                 transpose_block(bi)
-            issue_loads()
+            issue_loads(LOADS_PER_SLOT if s >= 0 else 2)

@@ -15,6 +15,7 @@ SILU = mybir.ActivationFunctionType.Silu
 MULT = mybir.AluOpType.mult
 
 P = 128
+QUADRANT = 32
 K_PASS = 512
 CHUNK = 512
 HALF = 256
@@ -22,21 +23,15 @@ H_PASSES = H // K_PASS
 R_PASSES = R // K_PASS
 TOKEN_CHUNKS = T // CHUNK
 TOKEN_TILES = T // P
+CHUNK_WIDTHS = (CHUNK,) * (I // CHUNK) + (I % CHUNK,)
 
-CHUNK_WIDTHS = (512,) * 10 + (256,)
-RAW_BUFS = 3
-HEAD_SLOTS = 5
-STAGE1_SLOTS = 8 * TOKEN_CHUNKS
-FIRST_DVE_CHUNK = 1
-TWO_QUEUES = True
-INTERLEAVE_ON_SCALAR_EVERY = 2
-EARLY_SLOTS = (-5, -4, -3, -2, -1, 0, 1, 2, 3, 4, 5, 6, 8, 10, 13, 15)
-CHUNK0_SLOTS = (17, 19, 21, 23, 25, 26, 27, 28)
+LEAD_STEPS = 5
+P_STEPS = 8 * TOKEN_CHUNKS
+EARLY_STEPS = (-5, -4, -3, -2, -1, 0, 1, 2, 3, 4, 5, 6, 8, 10, 13, 15)
+FIRST_CHUNK_STEPS = (17, 19, 21, 23, 25, 26, 27, 28)
+UNIT_LEAD = 18
 UNIT_SPAN = 15
-UNIT_LEAD = 19
-NARROW_P = False
-LOADS_PER_SLOT = 1
-SORT_ON_SCALAR_EVERY = 1000
+RAW_BUFS = 3
 
 
 def tile_merge_mixtralsparsemoeblock_pa_l_kernel(tc, x, Wmean1, Wmean3, du1, dv1, du3, dv3, out):
@@ -68,108 +63,103 @@ def tile_merge_mixtralsparsemoeblock_pa_l_kernel(tc, x, Wmean1, Wmean3, du1, dv1
         for ci in range(len(CHUNK_WIDTHS)):
             chunk_start.append(sum(CHUNK_WIDTHS[:ci]))
 
-        jobs = []
-        blocks = []
+        operands = []
+        pieces = []
         plan = {}
-        uses_left = {}
+        reads_left = {}
 
-        def push(stage, slot, item):
-            if (stage, slot) not in plan:
-                plan[(stage, slot)] = []
-            plan[(stage, slot)].append(item)
+        def push(stage, step, item):
+            if (stage, step) not in plan:
+                plan[(stage, step)] = []
+            plan[(stage, step)].append(item)
 
-        def add_tensor_job(sources, passes, key, slots):
-            jb = len(jobs)
-            jobs.append((sources, passes, key, "pe", HALF * len(sources)))
-            uses_left[jb] = [passes * len(sources)]
-            for b in range(len(sources)):
+        def plan_tensor_way(sources, passes, key, steps):
+            op = len(operands)
+            operands.append((sources, passes, key, "tensor", HALF * len(sources)))
+            reads_left[op] = [passes * len(sources)]
+            for half in range(len(sources)):
                 for g in range(passes):
-                    bi = len(blocks)
-                    blocks.append((jb, b, g))
-                    push("sort", slots[b], bi)
-                    push("T", slots[b], bi)
+                    pc = len(pieces)
+                    pieces.append((op, half, g))
+                    push("sort", steps[half], pc)
+                    push("transpose", steps[half], pc)
                     if key[0] != "dv":
-                        push("Q", slots[b] + 1, bi)
-                    elif b == 1:
-                        push("Qwide", slots[b] + 1, (key, g))
+                        push("quantize", steps[half] + 1, pc)
+                    elif half == 1:
+                        push("quantize dv", steps[half] + 1, (key, g))
 
-        def add_vector_job(sources, passes, key, rows, slots):
-            jb = len(jobs)
-            jobs.append((sources, passes, key, "dve", rows))
-            uses_left[jb] = [passes]
+        def plan_vector_way(sources, passes, key, rows, steps):
+            op = len(operands)
+            operands.append((sources, passes, key, "vector", rows))
+            reads_left[op] = [passes]
             for g in range(passes):
-                bi = len(blocks)
-                blocks.append((jb, 0, g))
-                push("S", slots[g], bi)
-                push("V", slots[g] + 1, bi)
-                push("I", slots[g] + 2, bi)
-                push("Q", slots[g] + 3, bi)
+                pc = len(pieces)
+                pieces.append((op, 0, g))
+                push("quadrant sort", steps[g], pc)
+                push("quadrant transpose", steps[g] + 1, pc)
+                push("interleave", steps[g] + 2, pc)
+                push("quantize", steps[g] + 3, pc)
 
-        def slabs(ap):
-            return ap.rearrange("(b j p) k -> b p j k", j=2, p=P)
-
-        def dv_slabs(ap, gr):
-            return ap.rearrange("(b j g r) k -> g b r j k", b=2, j=2, g=R_PASSES)[gr]
-
-        def halves_of(view, n):
+        def split(view, n):
             parts = []
-            for b in range(n):
-                parts.append(view[b])
+            for k in range(n):
+                parts.append(view[k])
             return parts
 
-        def quadrants_of(ap):
-            view = ap.rearrange("(bb i) (q w) -> q i bb w", i=32, q=4)
-            return halves_of(view, 4)
+        def slabs(rows):
+            return split(rows.rearrange("(b j p) k -> b p j k", j=2, p=P), rows.shape[0] // HALF)
 
-        add_tensor_job(halves_of(slabs(x[0:CHUNK, :]), 2), H_PASSES, ("x", 0), EARLY_SLOTS[0:2])
+        def dv_slabs(dv, gr):
+            return split(dv.rearrange("(b j g r) k -> g b r j k", b=2, j=2, g=R_PASSES)[gr], 2)
+
+        def quadrants(rows):
+            return split(rows.rearrange("(bb i) (q w) -> q i bb w", i=QUADRANT, q=4), 4)
+
+        plan_tensor_way(slabs(x[0:CHUNK, :]), H_PASSES, ("x", 0), EARLY_STEPS[0:2])
         for i in range(2):
             for gr in range(R_PASSES):
                 k = 2 + 4 * i + 2 * gr
-                add_tensor_job(halves_of(dv_slabs(dv_in[i], gr), 2), H_PASSES, ("dv", i, gr), EARLY_SLOTS[k : k + 2])
+                plan_tensor_way(dv_slabs(dv_in[i], gr), H_PASSES, ("dv", i, gr), EARLY_STEPS[k : k + 2])
         for c in range(1, TOKEN_CHUNKS):
-            add_tensor_job(
-                halves_of(slabs(x[CHUNK * c : CHUNK * (c + 1), :]), 2),
-                H_PASSES,
-                ("x", c),
-                EARLY_SLOTS[8 + 2 * c : 10 + 2 * c],
+            plan_tensor_way(
+                slabs(x[CHUNK * c : CHUNK * (c + 1), :]), H_PASSES, ("x", c), EARLY_STEPS[8 + 2 * c : 10 + 2 * c]
             )
 
         for ci in range(len(CHUNK_WIDTHS)):
             width = CHUNK_WIDTHS[ci]
-            base = STAGE1_SLOTS + TOKEN_TILES * ci
-            seen = 0
-            count = 0
+            first_tile_step = P_STEPS + TOKEN_TILES * ci
+            n_passes = 0
+            n_operands = 0
             for kind in ("w", "du"):
                 passes = H_PASSES if kind == "w" else R_PASSES
                 for i in range(2):
                     rows = weights[kind][i][chunk_start[ci] : chunk_start[ci] + width, :]
-                    if ci < FIRST_DVE_CHUNK:
-                        add_tensor_job(
-                            halves_of(slabs(rows), width // HALF),
-                            passes,
-                            (kind, ci, i),
-                            CHUNK0_SLOTS[2 * count : 2 * count + 2],
+                    if ci == 0:
+                        plan_tensor_way(
+                            slabs(rows), passes, (kind, ci, i), FIRST_CHUNK_STEPS[2 * n_operands : 2 * n_operands + 2]
                         )
                     else:
-                        slots = []
+                        steps = []
                         for g in range(passes):
-                            slots.append(base - UNIT_LEAD + (UNIT_SPAN * seen) // (2 * (H_PASSES + R_PASSES)))
-                            seen += 1
-                        add_vector_job(quadrants_of(rows), passes, (kind, ci, i), width, slots)
-                    count += 1
+                            steps.append(
+                                first_tile_step - UNIT_LEAD + (UNIT_SPAN * n_passes) // (2 * (H_PASSES + R_PASSES))
+                            )
+                            n_passes += 1
+                        plan_vector_way(quadrants(rows), passes, (kind, ci, i), width, steps)
+                    n_operands += 1
 
         raw_of = {}
-        stg_of = {}
-        v1_of = {}
-        grp_of = {}
-        wide_of = {}
-        units = {}
-        done = {}
+        sorted_of = {}
+        turned_of = {}
+        grouped_of = {}
+        dv_grouped_of = {}
+        codes_of = {}
+        read_out = {}
         next_load = [0]
         waiting_loads = [[], []]
 
-        def unit_tiles(key, g):
-            if (key, g) not in units:
+        def codes_tiles(key, g):
+            if (key, g) not in codes_of:
                 if key[0] == "x" or key[0] == "p":
                     label = "%s%d" % (key[0], 100 * key[1] + 10 * key[-1] + g)
                     codes = keep.tile([P, CHUNK], U32, name="c_" + label, align_bytes=64)
@@ -177,63 +167,68 @@ def tile_merge_mixtralsparsemoeblock_pa_l_kernel(tc, x, Wmean1, Wmean3, du1, dv1
                 else:
                     codes = wcp.tile([P, CHUNK], U32, name="wcodes", tag="wcodes", align_bytes=64)
                     scales = wcp.tile([P, CHUNK], U8, name="wscales", tag="wscales", align_bytes=64)
-                units[(key, g)] = (codes, scales)
-            return units[(key, g)]
+                codes_of[(key, g)] = (codes, scales)
+            return codes_of[(key, g)]
 
-        def issue_loads(limit):
-            while next_load[0] < len(jobs) and (next_load[0] < RAW_BUFS or (next_load[0] - RAW_BUFS) in done):
-                jb = next_load[0]
-                sources, passes, key, path, rows = jobs[jb]
-                if path == "pe":
+        def start_loads(limit):
+            while next_load[0] < len(operands) and (next_load[0] < RAW_BUFS or (next_load[0] - RAW_BUFS) in read_out):
+                op = next_load[0]
+                sources, passes, key, way, rows = operands[op]
+                if way == "tensor":
                     raw = rawp.tile([P, rows // P, passes * K_PASS], BF16, name="raw", tag="raw")
-                    for b in range(len(sources)):
-                        waiting_loads[0].append((raw[:, 2 * b : 2 * b + 2, :], sources[b]))
+                    for half in range(len(sources)):
+                        waiting_loads[0].append((raw[:, 2 * half : 2 * half + 2, :], sources[half]))
                 else:
-                    raw = rawp.tile([P, rows // 32, passes * K_PASS // 4], BF16, name="raw", tag="raw")
-                    for q in (0, 2, 1, 3):
-                        lane = 1 if (TWO_QUEUES and q >= 2) else 0
-                        waiting_loads[lane].append((raw[32 * q : 32 * (q + 1), :, :], sources[q]))
-                raw_of[jb] = raw
-                next_load[0] = jb + 1
+                    raw = rawp.tile([P, rows // QUADRANT, passes * K_PASS // 4], BF16, name="raw", tag="raw")
+                    for q in range(4):
+                        waiting_loads[q // 2].append((raw[QUADRANT * q : QUADRANT * (q + 1), :, :], sources[q]))
+                raw_of[op] = raw
+                next_load[0] = op + 1
             for lane in range(2):
                 queue = nc.scalar if lane == 1 else nc.sync
                 for item in waiting_loads[lane][:limit]:
                     queue.dma_start(out=item[0], in_=item[1])
                 waiting_loads[lane] = waiting_loads[lane][limit:]
 
-        def consumed(jb):
-            uses_left[jb][0] -= 1
-            if uses_left[jb][0] == 0:
-                done[jb] = True
+        def count_read(op):
+            reads_left[op][0] -= 1
+            if reads_left[op][0] == 0:
+                read_out[op] = True
 
-        def sort_block(bi):
-            jb, b, g = blocks[bi]
-            words = raw_of[jb][:].bitcast(F32)
+        def sort_words(pc):
+            op, half, g = pieces[pc]
+            words = raw_of[op][:].bitcast(F32)
             srt = epi.tile([P, 2, 2, P], F32, name="srt", tag="w2k")
             for j in range(2):
-                dst = srt[:, j, :, :].rearrange("p u (q jj) -> p u q jj", q=4)
-                src = words[:, 2 * b + j, :].rearrange("p (q g jj u) -> p g u q jj", q=4, g=jobs[jb][1], u=2)[:, g]
-                if bi % SORT_ON_SCALAR_EVERY == 0:
-                    nc.scalar.copy(out=dst, in_=src)
+                if operands[op][1] == H_PASSES:
+                    nc.vector.tensor_copy(
+                        out=srt[:, j, :, :].rearrange("p u (o jp) -> p u o jp", jp=8),
+                        in_=words[:, 2 * half + j, :].rearrange("p (o g u jp) -> p g u o jp", g=H_PASSES, u=2, jp=8)[:, g],
+                    )
                 else:
-                    nc.vector.tensor_copy(out=dst, in_=src)
-            stg_of[bi] = srt
-            consumed(jb)
+                    nc.vector.tensor_copy(
+                        out=srt[:, j, :, :].rearrange("p u (q jj) -> p u q jj", q=4),
+                        in_=words[:, 2 * half + j, :].rearrange(
+                            "p (q g jj u) -> p g u q jj", q=4, g=operands[op][1], u=2
+                        )[:, g],
+                    )
+            sorted_of[pc] = srt
+            count_read(op)
 
-        def transpose_block(bi):
-            jb, b, g = blocks[bi]
-            key = jobs[jb][2]
+        def transpose_words(pc):
+            op, half, g = pieces[pc]
+            key = operands[op][2]
             tp = tpp.tile([P, 2, 2, P], F32, name="tp", tag="tp")
             for j in range(2):
                 for u in range(2):
-                    nc.tensor.transpose(tp[:, j, u, :], stg_of[bi][:, j, u, :], ident[:])
+                    nc.tensor.transpose(tp[:, j, u, :], sorted_of[pc][:, j, u, :], ident[:])
             if key[0] == "dv":
-                if (key, g) not in wide_of:
-                    wide_of[(key, g)] = grpp.tile([P, CHUNK, 4], BF16, name="gdv", tag="grp", align_bytes=64)
-                view = wide_of[(key, g)][:].bitcast(F32).rearrange("p (t qq jj) u -> p t qq jj u", t=4, qq=4)
+                if (key, g) not in dv_grouped_of:
+                    dv_grouped_of[(key, g)] = grpp.tile([P, CHUNK, 4], BF16, name="gdv", tag="grp", align_bytes=64)
+                view = dv_grouped_of[(key, g)][:].bitcast(F32).rearrange("p (t qq jj) u -> p t qq jj u", t=4, qq=4)
                 for j in range(2):
                     nc.scalar.copy(
-                        out=view[:, :, 2 * b + j, :, :],
+                        out=view[:, :, 2 * half + j, :, :],
                         in_=tp[:, j, :, :].rearrange("p u (jj t) -> p t jj u", t=4),
                     )
             else:
@@ -242,53 +237,62 @@ def tile_merge_mixtralsparsemoeblock_pa_l_kernel(tc, x, Wmean1, Wmean3, du1, dv1
                     out=grp[:].bitcast(F32).rearrange("p (j r) u -> p j r u", j=2),
                     in_=tp[:].rearrange("p j u r -> p j r u"),
                 )
-                grp_of[bi] = grp
+                grouped_of[pc] = grp
 
-        def presort_unit(bi):
-            jb, b, g = blocks[bi]
-            words = raw_of[jb][:].bitcast(F32)
-            s1 = stgp.tile([P, 2, jobs[jb][4] // 32, 32], F32, name="s1", tag="s1", align_bytes=64)
-            nc.scalar.copy(out=s1[:], in_=words[:, :, 64 * g : 64 * (g + 1)].rearrange("p bb (j u) -> p u bb j", u=2))
-            stg_of[bi] = s1
-            consumed(jb)
-
-        def vector_transpose_unit(bi):
-            v1 = stgp.tile([P, 2 * jobs[blocks[bi][0]][4]], F32, name="v1", tag="v1", bufs=2, align_bytes=64)
-            nc.vector.transpose(out=v1[:], in_=stg_of[bi][:].rearrange("p u bb j -> p (u bb j)"))
-            v1_of[bi] = v1
-
-        def interleave_unit(bi):
-            grp = grpp.tile([P, jobs[blocks[bi][0]][4], 4], BF16, name="grp", tag="grp", align_bytes=64)
-            if bi % INTERLEAVE_ON_SCALAR_EVERY == 0:
-                nc.scalar.copy(out=grp[:].bitcast(F32), in_=v1_of[bi][:].rearrange("p (u r) -> p r u", u=2))
+        def sort_quadrant_words(pc):
+            op, half, g = pieces[pc]
+            words = raw_of[op][:].bitcast(F32)
+            s1 = stgp.tile([P, 2, operands[op][4] // QUADRANT, QUADRANT], F32, name="s1", tag="s1", align_bytes=64)
+            if operands[op][1] == H_PASSES:
+                flat = raw_of[op][:].rearrange("p bb w -> p (bb w)").bitcast(F32)
+                nc.scalar.copy(
+                    out=s1[:].rearrange("p u bb (s jp) -> p u (bb s) jp", jp=8),
+                    in_=flat.rearrange("p (bs g u jp) -> p g u bs jp", g=H_PASSES, u=2, jp=8)[:, g],
+                )
             else:
-                nc.vector.tensor_copy(out=grp[:].bitcast(F32), in_=v1_of[bi][:].rearrange("p (u r) -> p r u", u=2))
-            grp_of[bi] = grp
+                nc.scalar.copy(
+                    out=s1[:], in_=words[:, :, 64 * g : 64 * (g + 1)].rearrange("p bb (j u) -> p u bb j", u=2)
+                )
+            sorted_of[pc] = s1
+            count_read(op)
 
-        def quantize_block(bi):
-            jb, b, g = blocks[bi]
-            codes, scales = unit_tiles(jobs[jb][2], g)
-            n = HALF if jobs[jb][3] == "pe" else jobs[jb][4]
-            cols = slice(n * b, n * (b + 1))
+        def transpose_in_quadrants(pc):
+            v1 = stgp.tile([P, 2 * operands[pieces[pc][0]][4]], F32, name="v1", tag="v1", bufs=2, align_bytes=64)
+            nc.vector.transpose(out=v1[:], in_=sorted_of[pc][:].rearrange("p u bb j -> p (u bb j)"))
+            turned_of[pc] = v1
+
+        def interleave_words(pc):
+            grp = grpp.tile([P, operands[pieces[pc][0]][4], 4], BF16, name="grp", tag="grp", align_bytes=64)
+            if pc % 2 == 0:
+                nc.scalar.copy(out=grp[:].bitcast(F32), in_=turned_of[pc][:].rearrange("p (u r) -> p r u", u=2))
+            else:
+                nc.vector.tensor_copy(out=grp[:].bitcast(F32), in_=turned_of[pc][:].rearrange("p (u r) -> p r u", u=2))
+            grouped_of[pc] = grp
+
+        def quantize_piece(pc):
+            op, half, g = pieces[pc]
+            codes, scales = codes_tiles(operands[op][2], g)
+            n = HALF if operands[op][3] == "tensor" else operands[op][4]
+            cols = slice(n * half, n * (half + 1))
             nc.vector.quantize_mx(
                 out=codes[:, cols].bitcast(FP8X4),
                 scales=scales[:, cols],
-                in_=grp_of[bi][:].rearrange("p r t -> p (r t)"),
+                in_=grouped_of[pc][:].rearrange("p r t -> p (r t)"),
             )
 
-        def quantize_wide(tile_ap, key, g):
-            codes, scales = unit_tiles(key, g)
+        def quantize_pass(grouped, key, g):
+            codes, scales = codes_tiles(key, g)
             nc.vector.quantize_mx(
-                out=codes[:].bitcast(FP8X4), scales=scales[:], in_=tile_ap[:].rearrange("p c t -> p (c t)")
+                out=codes[:].bitcast(FP8X4), scales=scales[:], in_=grouped[:].rearrange("p c t -> p (c t)")
             )
 
-        def p_groups(i, gr, c, h, pst):
-            for t in (2 * h, 2 * h + 1):
+        def p_banks(i, gr, c, t_pair, rounded):
+            for t in (2 * t_pair, 2 * t_pair + 1):
                 cols = slice(P * t, P * (t + 1))
                 acc = accp.tile([P, CHUNK], F32, name="acc", tag="acc")
                 for g in range(H_PASSES):
-                    dc, ds = units[(("dv", i, gr), g)]
-                    xc, xs = units[(("x", c), g)]
+                    dc, ds = codes_of[(("dv", i, gr), g)]
+                    xc, xs = codes_of[(("x", c), g)]
                     nc.tensor.matmul_mx(
                         out=acc[:],
                         lhsT=dc[:, cols].bitcast(FP8X4),
@@ -298,29 +302,9 @@ def tile_merge_mixtralsparsemoeblock_pa_l_kernel(tc, x, Wmean1, Wmean3, du1, dv1
                         start=(g == 0),
                         stop=(g == H_PASSES - 1),
                     )
-                nc.scalar.copy(out=pst[:, t, :], in_=acc[:])
+                nc.scalar.copy(out=rounded[:, t, :], in_=acc[:])
 
-        def p_banks(i, gr, c, h, pg):
-            for tq in (2 * h, 2 * h + 1):
-                tok = slice(P * tq, P * (tq + 1))
-                acc = accp.tile([P, 4, P], F32, name="acc", tag="acc")
-                for t in range(4):
-                    cols = slice(P * t, P * (t + 1))
-                    for g in range(H_PASSES):
-                        dc, ds = units[(("dv", i, gr), g)]
-                        xc, xs = units[(("x", c), g)]
-                        nc.tensor.matmul_mx(
-                            out=acc[:, t, :],
-                            lhsT=dc[:, cols].bitcast(FP8X4),
-                            lhsT_scale=ds[:, cols],
-                            rhs=xc[:, tok].bitcast(FP8X4),
-                            rhs_scale=xs[:, tok],
-                            start=(g == 0),
-                            stop=(g == H_PASSES - 1),
-                        )
-                nc.scalar.copy(out=pg[:, tok, :], in_=acc[:].rearrange("p t c -> p c t"))
-
-        def output_tile(ci, m):
+        def z_tile(ci, m):
             width = CHUNK_WIDTHS[ci]
             c = m // 4
             tok = slice(P * (m % 4), P * (m % 4 + 1))
@@ -328,20 +312,20 @@ def tile_merge_mixtralsparsemoeblock_pa_l_kernel(tc, x, Wmean1, Wmean3, du1, dv1
             for i in range(2):
                 pairs = []
                 for g in range(H_PASSES):
-                    pairs.append((units[(("x", c), g)], units[(("w", ci, i), g)]))
+                    pairs.append((codes_of[(("x", c), g)], codes_of[(("w", ci, i), g)]))
                 for gr in range(R_PASSES):
-                    pairs.append((units[(("p", i, gr), c)], units[(("du", ci, i), gr)]))
+                    pairs.append((codes_of[(("p", i, gr), c)], codes_of[(("du", ci, i), gr)]))
                 acc = accp.tile([P, CHUNK], F32, name="acc", tag="acc")
-                for q in range(len(pairs)):
-                    (ac, asc), (wc, wsc) = pairs[q]
+                for n in range(len(pairs)):
+                    (ac, asc), (wc, wsc) = pairs[n]
                     nc.tensor.matmul_mx(
                         out=acc[:, :width],
                         lhsT=ac[:, tok].bitcast(FP8X4),
                         lhsT_scale=asc[:, tok],
                         rhs=wc[:, :width].bitcast(FP8X4),
                         rhs_scale=wsc[:, :width],
-                        start=(q == 0),
-                        stop=(q == len(pairs) - 1),
+                        start=(n == 0),
+                        stop=(n == len(pairs) - 1),
                     )
                 banks.append(acc)
             sg = epi.tile([P, CHUNK], F32, name="sg", tag="w2k")
@@ -351,53 +335,44 @@ def tile_merge_mixtralsparsemoeblock_pa_l_kernel(tc, x, Wmean1, Wmean3, du1, dv1
             first = chunk_start[ci]
             nc.sync.dma_start(out=out[P * m : P * (m + 1), first : first + width], in_=z[:, :width])
 
-        issue_loads(2 * RAW_BUFS)
-        waiting_p = []
-        full_p = []
-        late_p = []
-        pst = None
-        for s in range(-HEAD_SLOTS, STAGE1_SLOTS + TOKEN_TILES * len(CHUNK_WIDTHS)):
-            for bi in plan.get(("V", s), []):
-                vector_transpose_unit(bi)
-            for bi in plan.get(("I", s), []):
-                interleave_unit(bi)
-            for bi in plan.get(("sort", s), []):
-                sort_block(bi)
-            for bi in plan.get(("S", s), []):
-                presort_unit(bi)
-            if 0 <= s < STAGE1_SLOTS:
-                c = s // 8
-                i = (s % 8) // 4
-                gr = ((s % 8) // 2) % 2
-                h = s % 2
-                if NARROW_P:
-                    if h == 0:
-                        pst = pstp.tile([P, CHUNK, 4], BF16, name="pg", tag="pg", align_bytes=64)
-                    p_banks(i, gr, c, h, pst)
-                    if h == 1:
-                        late_p.append((pst, ("p", i, gr), c))
-                else:
-                    if h == 0:
-                        pst = pstp.tile([P, 4, CHUNK], BF16, name="pst", tag="pst")
-                    p_groups(i, gr, c, h, pst)
-                    if h == 1:
-                        full_p.append((pst, ("p", i, gr), c))
-            elif s >= STAGE1_SLOTS:
-                output_tile((s - STAGE1_SLOTS) // TOKEN_TILES, (s - STAGE1_SLOTS) % TOKEN_TILES)
-            for bi in plan.get(("Q", s), []):
-                quantize_block(bi)
-            for item in plan.get(("Qwide", s), []):
-                quantize_wide(wide_of[item], item[0], item[1])
-            for item in waiting_p:
-                quantize_wide(item[0], item[1], item[2])
-            waiting_p = late_p
-            late_p = []
-            if len(full_p) > 0 and (s % 2 == 0 or s >= STAGE1_SLOTS):
-                item = full_p[0]
-                full_p = []
-                pg = pstp.tile([P, CHUNK, 4], BF16, name="pg", tag="pg", bufs=1, align_bytes=64)
-                nc.vector.tensor_copy(out=pg[:], in_=item[0][:].rearrange("p t c -> p c t"))
-                waiting_p.append((pg, item[1], item[2]))
-            for bi in plan.get(("T", s), []):
-                transpose_block(bi)
-            issue_loads(LOADS_PER_SLOT if s >= 0 else 2)
+        start_loads(2 * RAW_BUFS)
+        p_to_interleave = []
+        p_to_quantize = []
+        rounded = None
+        for step in range(-LEAD_STEPS, P_STEPS + TOKEN_TILES * len(CHUNK_WIDTHS)):
+            for pc in plan.get(("quadrant transpose", step), []):
+                transpose_in_quadrants(pc)
+            for pc in plan.get(("interleave", step), []):
+                interleave_words(pc)
+            for pc in plan.get(("sort", step), []):
+                sort_words(pc)
+            for pc in plan.get(("quadrant sort", step), []):
+                sort_quadrant_words(pc)
+            if 0 <= step < P_STEPS:
+                c = step // 8
+                i = (step % 8) // 4
+                gr = ((step % 8) // 2) % 2
+                t_pair = step % 2
+                if t_pair == 0:
+                    rounded = pstp.tile([P, 4, CHUNK], BF16, name="pst", tag="pst")
+                p_banks(i, gr, c, t_pair, rounded)
+                if t_pair == 1:
+                    p_to_interleave.append((rounded, ("p", i, gr), c))
+            elif step >= P_STEPS:
+                z_tile((step - P_STEPS) // TOKEN_TILES, (step - P_STEPS) % TOKEN_TILES)
+            for pc in plan.get(("quantize", step), []):
+                quantize_piece(pc)
+            for item in plan.get(("quantize dv", step), []):
+                quantize_pass(dv_grouped_of[item], item[0], item[1])
+            for item in p_to_quantize:
+                quantize_pass(item[0], item[1], item[2])
+            p_to_quantize = []
+            if len(p_to_interleave) > 0 and (step % 2 == 0 or step >= P_STEPS):
+                item = p_to_interleave[0]
+                p_to_interleave = []
+                grouped = pstp.tile([P, CHUNK, 4], BF16, name="pg", tag="pg", bufs=1, align_bytes=64)
+                nc.vector.tensor_copy(out=grouped[:], in_=item[0][:].rearrange("p t c -> p c t"))
+                p_to_quantize.append((grouped, item[1], item[2]))
+            for pc in plan.get(("transpose", step), []):
+                transpose_words(pc)
+            start_loads(1 if step >= 0 else 2)

from contextlib import ExitStack

import concourse.masks as masks
import concourse.mybir as mybir

T, H, I, R = 2048, 1536, 5376, 1024
FLOPS = 2 * T * (2 * H * I + 2 * H * R + 2 * R * I)

F32 = mybir.dt.float32
BF16 = mybir.dt.bfloat16
U32 = mybir.dt.uint32
U8 = mybir.dt.uint8
FP8X4 = mybir.dt.float8_e4m3fn_x4
SILU = mybir.ActivationFunctionType.Silu
MULT = mybir.AluOpType.mult

P = 128
QUADRANT = 32
K_PASS = 512
CHUNK = 512
HALF = 256
H_PASSES = H // K_PASS
R_PASSES = R // K_PASS
TOKEN_CHUNKS = T // CHUNK
TOKEN_TILES = T // P
CHUNK_WIDTHS = (CHUNK,) * (I // CHUNK) + (I % CHUNK,)

LEAD_STEPS = 5
P_STEPS = 8 * TOKEN_CHUNKS
EARLY_STEPS = (-5, -4, -3, -2, -1, 0, 1, 2, 3, 4, 5, 6, 8, 10, 13, 15)
FIRST_CHUNK_STEPS = (17, 19, 21, 23, 25, 26, 27, 28)
UNIT_LEAD = 18
UNIT_SPAN = 15
RAW_BUFS = 3


def tile_merge_mixtralsparsemoeblock_pa_l_kernel(tc, x, Wmean1, Wmean3, du1, dv1, du3, dv3, out):
    nc = tc.nc
    with ExitStack() as ctx:
        keep = ctx.enter_context(tc.tile_pool(name="keep", bufs=1))
        rawp = ctx.enter_context(tc.tile_pool(name="rawp", bufs=RAW_BUFS))
        grpp = ctx.enter_context(tc.tile_pool(name="grpp", bufs=6))
        wcp = ctx.enter_context(tc.tile_pool(name="wcp", bufs=22))
        pstp = ctx.enter_context(tc.tile_pool(name="pstp", bufs=2))
        stgp = ctx.enter_context(tc.tile_pool(name="stgp", bufs=3))
        epi = ctx.enter_context(tc.tile_pool(name="epi", bufs=7))
        tpp = ctx.enter_context(tc.psum_pool(name="tpp", bufs=4))
        accp = ctx.enter_context(tc.psum_pool(name="accp", bufs=4))

        ident = keep.tile([P, P], F32, name="ident")
        masks.make_identity(nc, ident[:])
        warm_in = keep.tile([P, 8], F32, name="warm_in")
        warm_out = keep.tile([P, 8], F32, name="warm_out")
        nc.vector.memset(warm_in[:], 0.0)
        nc.scalar.activation(out=warm_out[:], in_=warm_in[:], func=SILU)

        ctx.enter_context(tc.manual_schedule())

        weights = {"w": (Wmean1, Wmean3), "du": (du1, du3)}
        dv_in = (dv1, dv3)

        chunk_start = []
        for ci in range(len(CHUNK_WIDTHS)):
            chunk_start.append(sum(CHUNK_WIDTHS[:ci]))

        operands = []
        pieces = []
        plan = {}
        reads_left = {}

        def push(stage, step, item):
            if (stage, step) not in plan:
                plan[(stage, step)] = []
            plan[(stage, step)].append(item)

        def plan_tensor_way(sources, passes, key, steps):
            op = len(operands)
            operands.append((sources, passes, key, "tensor", HALF * len(sources)))
            reads_left[op] = [passes * len(sources)]
            for half in range(len(sources)):
                for g in range(passes):
                    pc = len(pieces)
                    pieces.append((op, half, g))
                    push("sort", steps[half], pc)
                    push("transpose", steps[half], pc)
                    if key[0] != "dv":
                        push("quantize", steps[half] + 1, pc)
                    elif half == 1:
                        push("quantize dv", steps[half] + 1, (key, g))

        def plan_vector_way(sources, passes, key, rows, steps):
            op = len(operands)
            operands.append((sources, passes, key, "vector", rows))
            reads_left[op] = [passes]
            for g in range(passes):
                pc = len(pieces)
                pieces.append((op, 0, g))
                push("quadrant sort", steps[g], pc)
                push("quadrant transpose", steps[g] + 1, pc)
                push("interleave", steps[g] + 2, pc)
                push("quantize", steps[g] + 3, pc)

        def split(view, n):
            parts = []
            for k in range(n):
                parts.append(view[k])
            return parts

        def slabs(rows):
            return split(rows.rearrange("(b j p) k -> b p j k", j=2, p=P), rows.shape[0] // HALF)

        def dv_slabs(dv, gr):
            return split(dv.rearrange("(b j g r) k -> g b r j k", b=2, j=2, g=R_PASSES)[gr], 2)

        def quadrants(rows):
            return split(rows.rearrange("(bb i) (q w) -> q i bb w", i=QUADRANT, q=4), 4)

        plan_tensor_way(slabs(x[0:CHUNK, :]), H_PASSES, ("x", 0), EARLY_STEPS[0:2])
        for i in range(2):
            for gr in range(R_PASSES):
                k = 2 + 4 * i + 2 * gr
                plan_tensor_way(dv_slabs(dv_in[i], gr), H_PASSES, ("dv", i, gr), EARLY_STEPS[k : k + 2])
        for c in range(1, TOKEN_CHUNKS):
            plan_tensor_way(
                slabs(x[CHUNK * c : CHUNK * (c + 1), :]), H_PASSES, ("x", c), EARLY_STEPS[8 + 2 * c : 10 + 2 * c]
            )

        for ci in range(len(CHUNK_WIDTHS)):
            width = CHUNK_WIDTHS[ci]
            first_tile_step = P_STEPS + TOKEN_TILES * ci
            n_passes = 0
            n_operands = 0
            for kind in ("w", "du"):
                passes = H_PASSES if kind == "w" else R_PASSES
                for i in range(2):
                    rows = weights[kind][i][chunk_start[ci] : chunk_start[ci] + width, :]
                    if ci == 0:
                        plan_tensor_way(
                            slabs(rows), passes, (kind, ci, i), FIRST_CHUNK_STEPS[2 * n_operands : 2 * n_operands + 2]
                        )
                    else:
                        steps = []
                        for g in range(passes):
                            steps.append(
                                first_tile_step - UNIT_LEAD + (UNIT_SPAN * n_passes) // (2 * (H_PASSES + R_PASSES))
                            )
                            n_passes += 1
                        plan_vector_way(quadrants(rows), passes, (kind, ci, i), width, steps)
                    n_operands += 1

        raw_of = {}
        sorted_of = {}
        turned_of = {}
        grouped_of = {}
        dv_grouped_of = {}
        codes_of = {}
        read_out = {}
        next_load = [0]
        waiting_loads = [[], []]

        def codes_tiles(key, g):
            if (key, g) not in codes_of:
                if key[0] == "x" or key[0] == "p":
                    label = "%s%d" % (key[0], 100 * key[1] + 10 * key[-1] + g)
                    codes = keep.tile([P, CHUNK], U32, name="c_" + label, align_bytes=64)
                    scales = keep.tile([P, CHUNK], U8, name="s_" + label, align_bytes=64)
                else:
                    codes = wcp.tile([P, CHUNK], U32, name="wcodes", tag="wcodes", align_bytes=64)
                    scales = wcp.tile([P, CHUNK], U8, name="wscales", tag="wscales", align_bytes=64)
                codes_of[(key, g)] = (codes, scales)
            return codes_of[(key, g)]

        def start_loads(limit):
            while next_load[0] < len(operands) and (next_load[0] < RAW_BUFS or (next_load[0] - RAW_BUFS) in read_out):
                op = next_load[0]
                sources, passes, key, way, rows = operands[op]
                if way == "tensor":
                    raw = rawp.tile([P, rows // P, passes * K_PASS], BF16, name="raw", tag="raw")
                    for half in range(len(sources)):
                        waiting_loads[0].append((raw[:, 2 * half : 2 * half + 2, :], sources[half]))
                else:
                    raw = rawp.tile([P, rows // QUADRANT, passes * K_PASS // 4], BF16, name="raw", tag="raw")
                    for q in range(4):
                        waiting_loads[q // 2].append((raw[QUADRANT * q : QUADRANT * (q + 1), :, :], sources[q]))
                raw_of[op] = raw
                next_load[0] = op + 1
            for lane in range(2):
                queue = nc.scalar if lane == 1 else nc.sync
                for item in waiting_loads[lane][:limit]:
                    queue.dma_start(out=item[0], in_=item[1])
                waiting_loads[lane] = waiting_loads[lane][limit:]

        def count_read(op):
            reads_left[op][0] -= 1
            if reads_left[op][0] == 0:
                read_out[op] = True

        def sort_words(pc):
            op, half, g = pieces[pc]
            words = raw_of[op][:].bitcast(F32)
            srt = epi.tile([P, 2, 2, P], F32, name="srt", tag="w2k")
            for j in range(2):
                if operands[op][1] == H_PASSES:
                    nc.vector.tensor_copy(
                        out=srt[:, j, :, :].rearrange("p u (o jp) -> p u o jp", jp=8),
                        in_=words[:, 2 * half + j, :].rearrange("p (o g u jp) -> p g u o jp", g=H_PASSES, u=2, jp=8)[:, g],
                    )
                else:
                    nc.vector.tensor_copy(
                        out=srt[:, j, :, :].rearrange("p u (q jj) -> p u q jj", q=4),
                        in_=words[:, 2 * half + j, :].rearrange(
                            "p (q g jj u) -> p g u q jj", q=4, g=operands[op][1], u=2
                        )[:, g],
                    )
            sorted_of[pc] = srt
            count_read(op)

        def transpose_words(pc):
            op, half, g = pieces[pc]
            key = operands[op][2]
            tp = tpp.tile([P, 2, 2, P], F32, name="tp", tag="tp")
            for j in range(2):
                for u in range(2):
                    nc.tensor.transpose(tp[:, j, u, :], sorted_of[pc][:, j, u, :], ident[:])
            if key[0] == "dv":
                if (key, g) not in dv_grouped_of:
                    dv_grouped_of[(key, g)] = grpp.tile([P, CHUNK, 4], BF16, name="gdv", tag="grp", align_bytes=64)
                view = dv_grouped_of[(key, g)][:].bitcast(F32).rearrange("p (t qq jj) u -> p t qq jj u", t=4, qq=4)
                for j in range(2):
                    nc.scalar.copy(
                        out=view[:, :, 2 * half + j, :, :],
                        in_=tp[:, j, :, :].rearrange("p u (jj t) -> p t jj u", t=4),
                    )
            else:
                grp = grpp.tile([P, HALF, 4], BF16, name="grp", tag="grp", align_bytes=64)
                nc.scalar.copy(
                    out=grp[:].bitcast(F32).rearrange("p (j r) u -> p j r u", j=2),
                    in_=tp[:].rearrange("p j u r -> p j r u"),
                )
                grouped_of[pc] = grp

        def sort_quadrant_words(pc):
            op, half, g = pieces[pc]
            words = raw_of[op][:].bitcast(F32)
            s1 = stgp.tile([P, 2, operands[op][4] // QUADRANT, QUADRANT], F32, name="s1", tag="s1", align_bytes=64)
            if operands[op][1] == H_PASSES:
                flat = raw_of[op][:].rearrange("p bb w -> p (bb w)").bitcast(F32)
                nc.scalar.copy(
                    out=s1[:].rearrange("p u bb (s jp) -> p u (bb s) jp", jp=8),
                    in_=flat.rearrange("p (bs g u jp) -> p g u bs jp", g=H_PASSES, u=2, jp=8)[:, g],
                )
            else:
                nc.scalar.copy(
                    out=s1[:], in_=words[:, :, 64 * g : 64 * (g + 1)].rearrange("p bb (j u) -> p u bb j", u=2)
                )
            sorted_of[pc] = s1
            count_read(op)

        def transpose_in_quadrants(pc):
            v1 = stgp.tile([P, 2 * operands[pieces[pc][0]][4]], F32, name="v1", tag="v1", bufs=2, align_bytes=64)
            nc.vector.transpose(out=v1[:], in_=sorted_of[pc][:].rearrange("p u bb j -> p (u bb j)"))
            turned_of[pc] = v1

        def interleave_words(pc):
            grp = grpp.tile([P, operands[pieces[pc][0]][4], 4], BF16, name="grp", tag="grp", align_bytes=64)
            if pc % 2 == 0:
                nc.scalar.copy(out=grp[:].bitcast(F32), in_=turned_of[pc][:].rearrange("p (u r) -> p r u", u=2))
            else:
                nc.vector.tensor_copy(out=grp[:].bitcast(F32), in_=turned_of[pc][:].rearrange("p (u r) -> p r u", u=2))
            grouped_of[pc] = grp

        def quantize_piece(pc):
            op, half, g = pieces[pc]
            codes, scales = codes_tiles(operands[op][2], g)
            n = HALF if operands[op][3] == "tensor" else operands[op][4]
            cols = slice(n * half, n * (half + 1))
            nc.vector.quantize_mx(
                out=codes[:, cols].bitcast(FP8X4),
                scales=scales[:, cols],
                in_=grouped_of[pc][:].rearrange("p r t -> p (r t)"),
            )

        def quantize_pass(grouped, key, g):
            codes, scales = codes_tiles(key, g)
            nc.vector.quantize_mx(
                out=codes[:].bitcast(FP8X4), scales=scales[:], in_=grouped[:].rearrange("p c t -> p (c t)")
            )

        def p_banks(i, gr, c, t_pair, rounded):
            for t in (2 * t_pair, 2 * t_pair + 1):
                cols = slice(P * t, P * (t + 1))
                acc = accp.tile([P, CHUNK], F32, name="acc", tag="acc")
                for g in range(H_PASSES):
                    dc, ds = codes_of[(("dv", i, gr), g)]
                    xc, xs = codes_of[(("x", c), g)]
                    nc.tensor.matmul_mx(
                        out=acc[:],
                        lhsT=dc[:, cols].bitcast(FP8X4),
                        lhsT_scale=ds[:, cols],
                        rhs=xc[:].bitcast(FP8X4),
                        rhs_scale=xs[:],
                        start=(g == 0),
                        stop=(g == H_PASSES - 1),
                    )
                nc.scalar.copy(out=rounded[:, t, :], in_=acc[:])

        def z_tile(ci, m):
            width = CHUNK_WIDTHS[ci]
            c = m // 4
            tok = slice(P * (m % 4), P * (m % 4 + 1))
            banks = []
            for i in range(2):
                pairs = []
                for g in range(H_PASSES):
                    pairs.append((codes_of[(("x", c), g)], codes_of[(("w", ci, i), g)]))
                for gr in range(R_PASSES):
                    pairs.append((codes_of[(("p", i, gr), c)], codes_of[(("du", ci, i), gr)]))
                acc = accp.tile([P, CHUNK], F32, name="acc", tag="acc")
                for n in range(len(pairs)):
                    (ac, asc), (wc, wsc) = pairs[n]
                    nc.tensor.matmul_mx(
                        out=acc[:, :width],
                        lhsT=ac[:, tok].bitcast(FP8X4),
                        lhsT_scale=asc[:, tok],
                        rhs=wc[:, :width].bitcast(FP8X4),
                        rhs_scale=wsc[:, :width],
                        start=(n == 0),
                        stop=(n == len(pairs) - 1),
                    )
                banks.append(acc)
            sg = epi.tile([P, CHUNK], F32, name="sg", tag="w2k")
            nc.scalar.activation(out=sg[:, :width], in_=banks[0][:, :width], func=SILU)
            z = epi.tile([P, CHUNK], F32, name="z", tag="w2k")
            nc.vector.tensor_tensor(out=z[:, :width], in0=banks[1][:, :width], in1=sg[:, :width], op=MULT)
            first = chunk_start[ci]
            nc.sync.dma_start(out=out[P * m : P * (m + 1), first : first + width], in_=z[:, :width])

        start_loads(2 * RAW_BUFS)
        p_to_interleave = []
        p_to_quantize = []
        rounded = None
        for step in range(-LEAD_STEPS, P_STEPS + TOKEN_TILES * len(CHUNK_WIDTHS)):
            for pc in plan.get(("quadrant transpose", step), []):
                transpose_in_quadrants(pc)
            for pc in plan.get(("interleave", step), []):
                interleave_words(pc)
            for pc in plan.get(("sort", step), []):
                sort_words(pc)
            for pc in plan.get(("quadrant sort", step), []):
                sort_quadrant_words(pc)
            if 0 <= step < P_STEPS:
                c = step // 8
                i = (step % 8) // 4
                gr = ((step % 8) // 2) % 2
                t_pair = step % 2
                if t_pair == 0:
                    rounded = pstp.tile([P, 4, CHUNK], BF16, name="pst", tag="pst")
                p_banks(i, gr, c, t_pair, rounded)
                if t_pair == 1:
                    p_to_interleave.append((rounded, ("p", i, gr), c))
            elif step >= P_STEPS:
                z_tile((step - P_STEPS) // TOKEN_TILES, (step - P_STEPS) % TOKEN_TILES)
            for pc in plan.get(("quantize", step), []):
                quantize_piece(pc)
            for item in plan.get(("quantize dv", step), []):
                quantize_pass(dv_grouped_of[item], item[0], item[1])
            for item in p_to_quantize:
                quantize_pass(item[0], item[1], item[2])
            p_to_quantize = []
            if len(p_to_interleave) > 0 and (step % 2 == 0 or step >= P_STEPS):
                item = p_to_interleave[0]
                p_to_interleave = []
                grouped = pstp.tile([P, CHUNK, 4], BF16, name="pg", tag="pg", bufs=1, align_bytes=64)
                nc.vector.tensor_copy(out=grouped[:], in_=item[0][:].rearrange("p t c -> p c t"))
                p_to_quantize.append((grouped, item[1], item[2]))
            for pc in plan.get(("transpose", step), []):
                transpose_words(pc)
            start_loads(1 if step >= 0 else 2)
